import numpy as np
import ml_dtypes


def mxq(x, axis, fmt="e4m3"):
    dtype, down = {"e4m3": (ml_dtypes.float8_e4m3fn, 7), "e5m2": (ml_dtypes.float8_e5m2, 14)}[fmt]
    v = np.moveaxis(np.asarray(x, np.float32).astype(ml_dtypes.bfloat16).astype(np.float64), axis, -1)
    blocks = v.reshape(v.shape[:-1] + (-1, 32))
    amax = np.abs(blocks).max(-1, keepdims=True)
    byte = np.maximum(np.where(amax > 0, np.frexp(amax)[1] - 1 + 127, 0) - down, 1)
    scale = np.exp2(byte - 127.0)
    codes = (blocks / scale).astype(np.float32).astype(dtype).astype(np.float64)
    return np.moveaxis((codes * scale).reshape(v.shape), -1, axis)


WIDE = False


def mx_kscale(k):
    if not WIDE:
        return np.ones(k)
    levels = np.array([10, -10, 5, -5, 0])
    a = np.random.permutation(np.resize(levels, k // 512 * 4)).reshape(k // 512, 4)
    idx = np.arange(k)
    return np.exp2(a[idx // 512, idx % 128 // 32])


BF16 = ml_dtypes.bfloat16


def bf(x):
    return np.asarray(x, np.float32).astype(BF16)


def f64(x):
    return np.asarray(x).astype(np.float64)


B, T, D, NH, HD, G, RD, F = 1, 640, 1024, 8, 128, 2, 16, 4096
LN_SCALE = 1.0 / np.sqrt(12.0)
EPS_RMS = 1e-6


def rmsnorm(x, eps):
    return x / np.sqrt(np.mean(np.square(x), axis=-1, keepdims=True) + eps)


def setup_inputs():
    t = np.exp2(np.round(np.log2(mx_kscale(F)) / 2))
    return {"x_mid": bf(np.random.standard_normal((B, T, D)) * np.random.uniform(0.5, 2.0, (B, T, 1))),
            "wfc": bf(np.random.standard_normal((F, D)) / (LN_SCALE * np.sqrt(D)) * t[:, None]),
            "wproj": bf(np.random.standard_normal((D, F)) / np.sqrt(F) / (t * t)[None, :]),
            "mlp_scale": bf(1.0 + 0.1 * np.random.standard_normal(D))}


def reference(x_mid, wfc, wproj, mlp_scale):
    x = f64(x_mid)
    h2 = rmsnorm(x, EPS_RMS) * LN_SCALE
    u = mxq(h2, 2, "e4m3") @ mxq(f64(wfc), 1, "e4m3").T
    act = np.square(np.where(u >= 0, u, 0.5 * u))
    return x + f64(mlp_scale) * (mxq(act, 2, "e4m3") @ mxq(f64(wproj), 1, "e4m3").T)

@@ -1,0 +1,239 @@
+from contextlib import ExitStack
+
+import concourse.mybir as mybir
+from concourse.masks import make_identity
+
+F32 = mybir.dt.float32
+BF16 = mybir.dt.bfloat16
+U32 = mybir.dt.uint32
+U8 = mybir.dt.uint8
+FP8X4 = mybir.dt.float8_e4m3fn_x4
+FUNC = mybir.ActivationFunctionType
+ALU = mybir.AluOpType
+
+P = 128
+T = 640
+D = 1024
+F = 4096
+K_PASS = 512
+BANK = 512
+D_PASSES = D // K_PASS
+F_GROUPS = F // K_PASS
+TOKEN_TILES = T // P
+GROUP_WORDS = 1024
+TOKEN_CHUNKS = ((0, 256), (256, 256), (512, 128))
+
+FLOPS = 2 * 2 * T * D * F
+
+
+def tile_block_pc_kernel(tc, x_mid, wfc, wproj, mlp_scale, out):
+    nc = tc.nc
+    x_rows = x_mid.flatten_outer_dims()
+    out_rows = out.flatten_outer_dims()
+
+    with ExitStack() as pools:
+        keep = pools.enter_context(tc.tile_pool(name="keep", bufs=1))
+        raw_pool = pools.enter_context(tc.tile_pool(name="raw", bufs=3))
+        stage_pool = pools.enter_context(tc.tile_pool(name="stage", bufs=3))
+        norm_pool = pools.enter_context(tc.tile_pool(name="norm", bufs=2))
+        act_pool = pools.enter_context(tc.tile_pool(name="act", bufs=3))
+        out_pool = pools.enter_context(tc.tile_pool(name="outp", bufs=4))
+        work = pools.enter_context(tc.psum_pool(name="work", bufs=4))
+        acc_pool = pools.enter_context(tc.psum_pool(name="acc", bufs=1))
+
+        ident_f32 = keep.tile([P, P], F32)
+        make_identity(nc, ident_f32[:])
+        ident_bf16 = keep.tile([P, P], BF16)
+        make_identity(nc, ident_bf16[:])
+        eps12 = keep.tile([P, 1], F32)
+        nc.vector.memset(eps12[:], 12.0e-6)
+        warm = keep.tile([P, 1], F32)
+        nc.scalar.activation(out=warm[:], in_=eps12[:], func=FUNC.Sqrt)
+
+        x_sb = keep.tile([P, TOKEN_TILES * D], BF16)
+        gain = keep.tile([P, D], BF16)
+        h_codes = keep.tile([P, D_PASSES * T], U32, align_bytes=64)
+        h_scales = keep.tile([P, D_PASSES * T], U8, align_bytes=64)
+        wfc_codes = keep.tile([P, F_GROUPS * GROUP_WORDS], U32, align_bytes=64)
+        wfc_scales = keep.tile([P, F_GROUPS * GROUP_WORDS], U8, align_bytes=64)
+        wproj_codes = keep.tile([P, F_GROUPS * GROUP_WORDS], U32, align_bytes=64)
+        wproj_scales = keep.tile([P, F_GROUPS * GROUP_WORDS], U8, align_bytes=64)
+        sumsq = keep.tile([P, TOKEN_TILES], F32)
+        rms = keep.tile([P, TOKEN_TILES], F32)
+        rstd = keep.tile([P, TOKEN_TILES], F32)
+
+        for tt in range(TOKEN_TILES):
+            nc.sync.dma_start(out=x_sb[:, tt * D : (tt + 1) * D], in_=x_rows[tt * P : (tt + 1) * P, :])
+        nc.gpsimd.dma_start(out=gain[:], in_=mlp_scale.partition_broadcast(P))
+
+        def quantise_h(tt):
+            x_tile = x_sb[:, tt * D : (tt + 1) * D]
+            squares = norm_pool.tile([P, D], BF16)
+            nc.scalar.activation(
+                out=squares[:], in_=x_tile, func=FUNC.Square, accum_out=sumsq[:, tt : tt + 1]
+            )
+            nc.scalar.activation(
+                out=rms[:, tt : tt + 1],
+                in_=sumsq[:, tt : tt + 1],
+                func=FUNC.Sqrt,
+                scale=12.0 / D,
+                bias=eps12[:],
+            )
+            nc.vector.reciprocal(out=rstd[:, tt : tt + 1], in_=rms[:, tt : tt + 1])
+            h_sorted = norm_pool.tile([P, D], BF16)
+            nc.vector.tensor_scalar(
+                out=h_sorted[:].rearrange("t (b e p) -> t b e p", b=4, e=2),
+                in0=x_tile.rearrange("t (b p e) -> t b e p", b=4, e=2),
+                scalar1=rstd[:, tt : tt + 1],
+                scalar2=None,
+                op0=ALU.mult,
+            )
+            h_bank = work.tile([P, 2 * BANK], BF16, tag="work")
+            for blk in range(D // P):
+                nc.tensor.transpose(
+                    h_bank[:, blk * P : (blk + 1) * P], h_sorted[:, blk * P : (blk + 1) * P], ident_bf16[:]
+                )
+            h_grouped = norm_pool.tile([P, D], BF16, align_bytes=64)
+            nc.vector.tensor_copy(
+                out=h_grouped[:].rearrange("p (c r t) -> p c r t", c=D_PASSES, t=4),
+                in_=h_bank[:].rearrange("p (c t r) -> p c r t", c=D_PASSES, t=4),
+            )
+            for c in range(D_PASSES):
+                cols = slice(c * T + tt * P, c * T + (tt + 1) * P)
+                nc.vector.quantize_mx(
+                    out=h_codes[:, cols].bitcast(FP8X4),
+                    scales=h_scales[:, cols],
+                    in_=h_grouped[:, c * K_PASS : (c + 1) * K_PASS],
+                )
+
+        for tt in range(TOKEN_TILES):
+            quantise_h(tt)
+
+        def quantise_weight_group(raw, codes, scales):
+            words = raw[:].bitcast(F32)
+            stage = stage_pool.tile([P, 4 * GROUP_WORDS], BF16, align_bytes=64)
+            stage_words = stage[:].bitcast(F32)
+            for b in range(4):
+                bank = work.tile([P, BANK], F32, tag="work")
+                for i in range(4):
+                    n = 4 * b + i
+                    nc.tensor.transpose(
+                        bank[:, i * P : (i + 1) * P], words[:, n * P : (n + 1) * P], ident_f32[:]
+                    )
+                nc.scalar.copy(
+                    out=stage_words[:, b * BANK : (b + 1) * BANK].rearrange(
+                        "p (r m u) -> p r m u", r=2, u=2
+                    ),
+                    in_=bank[:].rearrange("p (r u m) -> p r m u", r=2, u=2),
+                )
+            nc.vector.quantize_mx(out=codes.bitcast(FP8X4), scales=scales, in_=stage[:])
+
+        def prepare_weights(g):
+            group = slice(g * GROUP_WORDS, (g + 1) * GROUP_WORDS)
+            wfc_raw = raw_pool.tile([P, 4 * GROUP_WORDS], BF16)
+            nc.sync.dma_start(
+                out=wfc_raw[:].rearrange("p (u x) -> p u x", u=2),
+                in_=wfc[g * K_PASS : (g + 1) * K_PASS, :].rearrange("(u p e) d -> p u (e d)", u=2, e=2),
+            )
+            wproj_raw = raw_pool.tile([P, 4 * GROUP_WORDS], BF16)
+            nc.sync.dma_start(
+                out=wproj_raw[:].rearrange("p (r k) -> p r k", k=K_PASS),
+                in_=wproj[:, g * K_PASS : (g + 1) * K_PASS].rearrange("(r p) k -> p r k", p=P),
+            )
+            quantise_weight_group(wfc_raw, wfc_codes[:, group], wfc_scales[:, group])
+            quantise_weight_group(wproj_raw, wproj_codes[:, group], wproj_scales[:, group])
+
+        def hidden_group(tok0, n_tok, g):
+            square = act_pool.tile([P, 4 * n_tok], BF16, tag="square")
+            factor = act_pool.tile([P, 4 * n_tok], BF16, tag="factor")
+            for u in range(2):
+                u_bank = work.tile([P, 2 * n_tok], F32, tag="work")
+                for e in range(2):
+                    for c in range(D_PASSES):
+                        w_cols = slice(
+                            g * GROUP_WORDS + (4 * u + 2 * e + c) * P,
+                            g * GROUP_WORDS + (4 * u + 2 * e + c + 1) * P,
+                        )
+                        h_cols = slice(c * T + tok0, c * T + tok0 + n_tok)
+                        nc.tensor.matmul_mx(
+                            out=u_bank[:, e * n_tok : (e + 1) * n_tok],
+                            lhsT=wfc_codes[:, w_cols].bitcast(FP8X4),
+                            lhsT_scale=wfc_scales[:, w_cols],
+                            rhs=h_codes[:, h_cols].bitcast(FP8X4),
+                            rhs_scale=h_scales[:, h_cols],
+                            start=(c == 0),
+                            stop=(c == D_PASSES - 1),
+                        )
+                half = slice(u * 2 * n_tok, (u + 1) * 2 * n_tok)
+                pairs = u_bank[:].rearrange("p (e t) -> p t e", e=2)
+                nc.scalar.activation(
+                    out=square[:, half].rearrange("p (t e) -> p t e", e=2), in_=pairs, func=FUNC.Square
+                )
+                nc.vector.tensor_scalar(
+                    out=factor[:, half].rearrange("p (t e) -> p t e", e=2),
+                    in0=pairs,
+                    scalar1=0.0,
+                    scalar2=0.25,
+                    op0=ALU.is_ge,
+                    op1=ALU.max,
+                )
+            act_grouped = act_pool.tile([P, 4 * n_tok], BF16, tag="act_grouped", align_bytes=64)
+            nc.vector.tensor_tensor(
+                out=act_grouped[:].rearrange("p (t u e) -> p t u e", u=2, e=2),
+                in0=square[:].rearrange("p (u t e) -> p t u e", u=2, e=2),
+                in1=factor[:].rearrange("p (u t e) -> p t u e", u=2, e=2),
+                op=ALU.mult,
+            )
+            act_codes = act_pool.tile([P, n_tok], U32, tag="act_codes", align_bytes=64)
+            act_scales = act_pool.tile([P, n_tok], U8, tag="act_scales", align_bytes=64)
+            nc.vector.quantize_mx(out=act_codes[:].bitcast(FP8X4), scales=act_scales[:], in_=act_grouped[:])
+            return act_codes, act_scales
+
+        sums = {}
+
+        def project_group(tok0, n_tok, g, act_codes, act_scales):
+            for ti in range(n_tok // P):
+                for half in range(D // BANK):
+                    if g == 0:
+                        sums[(ti, half)] = acc_pool.tile(
+                            [P, BANK], F32, name="sum_%d_%d" % (ti, half), tag="sum_%d_%d" % (ti, half)
+                        )
+                    w_cols = slice(g * GROUP_WORDS + half * BANK, g * GROUP_WORDS + (half + 1) * BANK)
+                    nc.tensor.matmul_mx(
+                        out=sums[(ti, half)][:],
+                        lhsT=act_codes[:, ti * P : (ti + 1) * P].bitcast(FP8X4),
+                        lhsT_scale=act_scales[:, ti * P : (ti + 1) * P],
+                        rhs=wproj_codes[:, w_cols].bitcast(FP8X4),
+                        rhs_scale=wproj_scales[:, w_cols],
+                        start=(g == 0),
+                        stop=(g == F_GROUPS - 1),
+                    )
+            if g < F_GROUPS - 1:
+                return
+            for ti in range(n_tok // P):
+                tt = tok0 // P + ti
+                for half in range(D // BANK):
+                    d_cols = slice(half * BANK, (half + 1) * BANK)
+                    result = out_pool.tile([P, BANK], F32)
+                    nc.vector.tensor_tensor(
+                        out=result[:], in0=sums[(ti, half)][:], in1=gain[:, d_cols], op=ALU.mult
+                    )
+                    nc.gpsimd.tensor_tensor(
+                        out=result[:],
+                        in0=result[:],
+                        in1=x_sb[:, tt * D + half * BANK : tt * D + (half + 1) * BANK],
+                        op=ALU.add,
+                    )
+                    nc.sync.dma_start(out=out_rows[tt * P : (tt + 1) * P, d_cols], in_=result[:])
+
+        prepare_weights(0)
+        waiting = []
+        for tok0, n_tok in TOKEN_CHUNKS:
+            for g in range(F_GROUPS):
+                if tok0 == 0 and g + 1 < F_GROUPS:
+                    prepare_weights(g + 1)
+                codes_and_scales = hidden_group(tok0, n_tok, g)
+                if waiting:
+                    project_group(*waiting.pop())
+                waiting.append((tok0, n_tok, g) + codes_and_scales)
+        project_group(*waiting.pop())

@@ -33,13 +33,15 @@ def tile_block_pc_kernel(tc, x_mid, wfc, wproj, mlp_scale, out):
 
     with ExitStack() as pools:
         keep = pools.enter_context(tc.tile_pool(name="keep", bufs=1))
-        raw_pool = pools.enter_context(tc.tile_pool(name="raw", bufs=3))
+        wfc_pool = pools.enter_context(tc.tile_pool(name="wfc_raw", bufs=3))
+        wproj_pool = pools.enter_context(tc.tile_pool(name="wproj_raw", bufs=2))
         stage_pool = pools.enter_context(tc.tile_pool(name="stage", bufs=3))
         norm_pool = pools.enter_context(tc.tile_pool(name="norm", bufs=2))
         act_pool = pools.enter_context(tc.tile_pool(name="act", bufs=3))
         out_pool = pools.enter_context(tc.tile_pool(name="outp", bufs=4))
         work = pools.enter_context(tc.psum_pool(name="work", bufs=4))
         acc_pool = pools.enter_context(tc.psum_pool(name="acc", bufs=1))
+        pools.enter_context(tc.manual_schedule())
 
         ident_f32 = keep.tile([P, P], F32)
         make_identity(nc, ident_f32[:])
@@ -62,11 +64,10 @@ def tile_block_pc_kernel(tc, x_mid, wfc, wproj, mlp_scale, out):
         rms = keep.tile([P, TOKEN_TILES], F32)
         rstd = keep.tile([P, TOKEN_TILES], F32)
 
-        for tt in range(TOKEN_TILES):
+        def load_x(tt):
             nc.sync.dma_start(out=x_sb[:, tt * D : (tt + 1) * D], in_=x_rows[tt * P : (tt + 1) * P, :])
-        nc.gpsimd.dma_start(out=gain[:], in_=mlp_scale.partition_broadcast(P))
 
-        def quantise_h(tt):
+        def normalise(tt):
             x_tile = x_sb[:, tt * D : (tt + 1) * D]
             squares = norm_pool.tile([P, D], BF16)
             nc.scalar.activation(
@@ -88,6 +89,9 @@ def tile_block_pc_kernel(tc, x_mid, wfc, wproj, mlp_scale, out):
                 scalar2=None,
                 op0=ALU.mult,
             )
+            return h_sorted
+
+        def quantise_h(tt, h_sorted):
             h_bank = work.tile([P, 2 * BANK], BF16, tag="work")
             for blk in range(D // P):
                 nc.tensor.transpose(
@@ -106,44 +110,49 @@ def tile_block_pc_kernel(tc, x_mid, wfc, wproj, mlp_scale, out):
                     in_=h_grouped[:, c * K_PASS : (c + 1) * K_PASS],
                 )
 
-        for tt in range(TOKEN_TILES):
-            quantise_h(tt)
+        def load_wfc(g):
+            wfc_raw = wfc_pool.tile([P, 4 * GROUP_WORDS], BF16)
+            nc.sync.dma_start(
+                out=wfc_raw[:].rearrange("p (u x) -> p u x", u=2),
+                in_=wfc[g * K_PASS : (g + 1) * K_PASS, :].rearrange("(u p e) d -> p u (e d)", u=2, e=2),
+            )
+            words = wfc_raw[:].bitcast(F32)
+            return [words[:, n * P : (n + 1) * P] for n in range(16)]
 
-        def quantise_weight_group(raw, codes, scales):
-            words = raw[:].bitcast(F32)
+        def load_wproj_pair(g):
+            wproj_raw = wproj_pool.tile([P, 8 * GROUP_WORDS], BF16)
+            nc.sync.dma_start(
+                out=wproj_raw[:].rearrange("p (r k) -> p r k", k=2 * K_PASS),
+                in_=wproj[:, g * K_PASS : (g + 2) * K_PASS].rearrange("(r p) k -> p r k", p=P),
+            )
+            words = wproj_raw[:].bitcast(F32)
+            return [
+                [words[:, (4 * r + 2 * i + u) * P : (4 * r + 2 * i + u + 1) * P] for r in range(8) for u in range(2)]
+                for i in range(2)
+            ]
+
+        def transpose_weights(blocks, last_bank_on_vector):
             stage = stage_pool.tile([P, 4 * GROUP_WORDS], BF16, align_bytes=64)
             stage_words = stage[:].bitcast(F32)
             for b in range(4):
                 bank = work.tile([P, BANK], F32, tag="work")
                 for i in range(4):
-                    n = 4 * b + i
-                    nc.tensor.transpose(
-                        bank[:, i * P : (i + 1) * P], words[:, n * P : (n + 1) * P], ident_f32[:]
-                    )
-                nc.scalar.copy(
-                    out=stage_words[:, b * BANK : (b + 1) * BANK].rearrange(
-                        "p (r m u) -> p r m u", r=2, u=2
-                    ),
-                    in_=bank[:].rearrange("p (r u m) -> p r m u", r=2, u=2),
+                    nc.tensor.transpose(bank[:, i * P : (i + 1) * P], blocks[4 * b + i], ident_f32[:])
+                stage_part = stage_words[:, b * BANK : (b + 1) * BANK].rearrange(
+                    "p (r m u) -> p r m u", r=2, u=2
                 )
-            nc.vector.quantize_mx(out=codes.bitcast(FP8X4), scales=scales, in_=stage[:])
+                bank_view = bank[:].rearrange("p (r u m) -> p r m u", r=2, u=2)
+                if last_bank_on_vector and b == 3:
+                    nc.vector.tensor_copy(out=stage_part, in_=bank_view)
+                else:
+                    nc.scalar.copy(out=stage_part, in_=bank_view)
+            return stage
 
-        def prepare_weights(g):
+        def quantise_weights(stage, codes, scales, g):
             group = slice(g * GROUP_WORDS, (g + 1) * GROUP_WORDS)
-            wfc_raw = raw_pool.tile([P, 4 * GROUP_WORDS], BF16)
-            nc.sync.dma_start(
-                out=wfc_raw[:].rearrange("p (u x) -> p u x", u=2),
-                in_=wfc[g * K_PASS : (g + 1) * K_PASS, :].rearrange("(u p e) d -> p u (e d)", u=2, e=2),
-            )
-            wproj_raw = raw_pool.tile([P, 4 * GROUP_WORDS], BF16)
-            nc.sync.dma_start(
-                out=wproj_raw[:].rearrange("p (r k) -> p r k", k=K_PASS),
-                in_=wproj[:, g * K_PASS : (g + 1) * K_PASS].rearrange("(r p) k -> p r k", p=P),
-            )
-            quantise_weight_group(wfc_raw, wfc_codes[:, group], wfc_scales[:, group])
-            quantise_weight_group(wproj_raw, wproj_codes[:, group], wproj_scales[:, group])
+            nc.vector.quantize_mx(out=codes[:, group].bitcast(FP8X4), scales=scales[:, group], in_=stage[:])
 
-        def hidden_group(tok0, n_tok, g):
+        def hidden_matmul(tok0, n_tok, g):
             square = act_pool.tile([P, 4 * n_tok], BF16, tag="square")
             factor = act_pool.tile([P, 4 * n_tok], BF16, tag="factor")
             for u in range(2):
@@ -177,6 +186,9 @@ def tile_block_pc_kernel(tc, x_mid, wfc, wproj, mlp_scale, out):
                     op0=ALU.is_ge,
                     op1=ALU.max,
                 )
+            return square, factor
+
+        def quantise_act(n_tok, square, factor):
             act_grouped = act_pool.tile([P, 4 * n_tok], BF16, tag="act_grouped", align_bytes=64)
             nc.vector.tensor_tensor(
                 out=act_grouped[:].rearrange("p (t u e) -> p t u e", u=2, e=2),
@@ -226,13 +238,40 @@ def tile_block_pc_kernel(tc, x_mid, wfc, wproj, mlp_scale, out):
                     )
                     nc.sync.dma_start(out=out_rows[tt * P : (tt + 1) * P, d_cols], in_=result[:])
 
-        prepare_weights(0)
+        chunk_tiles = [list(range(tok0 // P, (tok0 + n_tok) // P)) for tok0, n_tok in TOKEN_CHUNKS]
+        for tt in chunk_tiles[0]:
+            load_x(tt)
+        wfc_blocks = load_wfc(0)
+        wproj_blocks = load_wproj_pair(0)
+        for tt in chunk_tiles[1] + chunk_tiles[2]:
+            load_x(tt)
+        nc.gpsimd.dma_start(out=gain[:], in_=mlp_scale.partition_broadcast(P))
+        sorted_tiles = [(tt, normalise(tt)) for tt in chunk_tiles[0]]
+        for tt, h_sorted in sorted_tiles:
+            quantise_h(tt, h_sorted)
+        quantise_weights(transpose_weights(wfc_blocks, False), wfc_codes, wfc_scales, 0)
+        quantise_weights(transpose_weights(wproj_blocks[0], True), wproj_codes, wproj_scales, 0)
+
         waiting = []
-        for tok0, n_tok in TOKEN_CHUNKS:
+        for ci, (tok0, n_tok) in enumerate(TOKEN_CHUNKS):
+            next_tiles = chunk_tiles[ci + 1] if ci + 1 < len(TOKEN_CHUNKS) else []
             for g in range(F_GROUPS):
-                if tok0 == 0 and g + 1 < F_GROUPS:
-                    prepare_weights(g + 1)
-                codes_and_scales = hidden_group(tok0, n_tok, g)
+                prepare = ci == 0 and g + 1 < F_GROUPS
+                if prepare:
+                    wfc_stage = transpose_weights(load_wfc(g + 1), False)
+                    quantise_weights(wfc_stage, wfc_codes, wfc_scales, g + 1)
+                    if (g + 1) % 2 == 0:
+                        wproj_blocks = load_wproj_pair(g + 1)
+                    wproj_stage = transpose_weights(wproj_blocks[(g + 1) % 2], True)
+                if g == 1:
+                    for tt, h_sorted in sorted_tiles:
+                        quantise_h(tt, h_sorted)
+                square, factor = hidden_matmul(tok0, n_tok, g)
+                if prepare:
+                    quantise_weights(wproj_stage, wproj_codes, wproj_scales, g + 1)
+                codes_and_scales = quantise_act(n_tok, square, factor)
+                if g == 0:
+                    sorted_tiles = [(tt, normalise(tt)) for tt in next_tiles]
                 if waiting:
                     project_group(*waiting.pop())
                 waiting.append((tok0, n_tok, g) + codes_and_scales)

@@ -23,6 +23,8 @@ TOKEN_TILES = T // P
 GROUP_WORDS = 1024
 TOKEN_CHUNKS = ((0, 256), (256, 256), (512, 128))
 
+LAG = 2
+
 FLOPS = 2 * 2 * T * D * F
 
 
@@ -37,11 +39,10 @@ def tile_block_pc_kernel(tc, x_mid, wfc, wproj, mlp_scale, out):
         wproj_pool = pools.enter_context(tc.tile_pool(name="wproj_raw", bufs=2))
         stage_pool = pools.enter_context(tc.tile_pool(name="stage", bufs=3))
         norm_pool = pools.enter_context(tc.tile_pool(name="norm", bufs=2))
-        act_pool = pools.enter_context(tc.tile_pool(name="act", bufs=3))
+        act_pool = pools.enter_context(tc.tile_pool(name="act", bufs=4))
         out_pool = pools.enter_context(tc.tile_pool(name="outp", bufs=4))
         work = pools.enter_context(tc.psum_pool(name="work", bufs=4))
         acc_pool = pools.enter_context(tc.psum_pool(name="acc", bufs=1))
-        pools.enter_context(tc.manual_schedule())
 
         ident_f32 = keep.tile([P, P], F32)
         make_identity(nc, ident_f32[:])
@@ -98,7 +99,7 @@ def tile_block_pc_kernel(tc, x_mid, wfc, wproj, mlp_scale, out):
                     h_bank[:, blk * P : (blk + 1) * P], h_sorted[:, blk * P : (blk + 1) * P], ident_bf16[:]
                 )
             h_grouped = norm_pool.tile([P, D], BF16, align_bytes=64)
-            nc.vector.tensor_copy(
+            nc.scalar.copy(
                 out=h_grouped[:].rearrange("p (c r t) -> p c r t", c=D_PASSES, t=4),
                 in_=h_bank[:].rearrange("p (c t r) -> p c r t", c=D_PASSES, t=4),
             )
@@ -155,17 +156,16 @@ def tile_block_pc_kernel(tc, x_mid, wfc, wproj, mlp_scale, out):
         def hidden_matmul(tok0, n_tok, g):
             square = act_pool.tile([P, 4 * n_tok], BF16, tag="square")
             factor = act_pool.tile([P, 4 * n_tok], BF16, tag="factor")
-            for u in range(2):
-                u_bank = work.tile([P, 2 * n_tok], F32, tag="work")
-                for e in range(2):
+            for ti in range(n_tok // P):
+                u_bank = work.tile([P, BANK], F32, tag="work")
+                for j in range(4):
                     for c in range(D_PASSES):
                         w_cols = slice(
-                            g * GROUP_WORDS + (4 * u + 2 * e + c) * P,
-                            g * GROUP_WORDS + (4 * u + 2 * e + c + 1) * P,
+                            g * GROUP_WORDS + (2 * j + c) * P, g * GROUP_WORDS + (2 * j + c + 1) * P
                         )
-                        h_cols = slice(c * T + tok0, c * T + tok0 + n_tok)
+                        h_cols = slice(c * T + tok0 + ti * P, c * T + tok0 + (ti + 1) * P)
                         nc.tensor.matmul_mx(
-                            out=u_bank[:, e * n_tok : (e + 1) * n_tok],
+                            out=u_bank[:, j * P : (j + 1) * P],
                             lhsT=wfc_codes[:, w_cols].bitcast(FP8X4),
                             lhsT_scale=wfc_scales[:, w_cols],
                             rhs=h_codes[:, h_cols].bitcast(FP8X4),
@@ -173,14 +173,14 @@ def tile_block_pc_kernel(tc, x_mid, wfc, wproj, mlp_scale, out):
                             start=(c == 0),
                             stop=(c == D_PASSES - 1),
                         )
-                half = slice(u * 2 * n_tok, (u + 1) * 2 * n_tok)
-                pairs = u_bank[:].rearrange("p (e t) -> p t e", e=2)
+                part = slice(ti * BANK, (ti + 1) * BANK)
+                words = u_bank[:].rearrange("p (j t) -> p t j", j=4)
                 nc.scalar.activation(
-                    out=square[:, half].rearrange("p (t e) -> p t e", e=2), in_=pairs, func=FUNC.Square
+                    out=square[:, part].rearrange("p (t j) -> p t j", j=4), in_=words, func=FUNC.Square
                 )
                 nc.vector.tensor_scalar(
-                    out=factor[:, half].rearrange("p (t e) -> p t e", e=2),
-                    in0=pairs,
+                    out=factor[:, part].rearrange("p (t j) -> p t j", j=4),
+                    in0=words,
                     scalar1=0.0,
                     scalar2=0.25,
                     op0=ALU.is_ge,
@@ -190,12 +190,7 @@ def tile_block_pc_kernel(tc, x_mid, wfc, wproj, mlp_scale, out):
 
         def quantise_act(n_tok, square, factor):
             act_grouped = act_pool.tile([P, 4 * n_tok], BF16, tag="act_grouped", align_bytes=64)
-            nc.vector.tensor_tensor(
-                out=act_grouped[:].rearrange("p (t u e) -> p t u e", u=2, e=2),
-                in0=square[:].rearrange("p (u t e) -> p t u e", u=2, e=2),
-                in1=factor[:].rearrange("p (u t e) -> p t u e", u=2, e=2),
-                op=ALU.mult,
-            )
+            nc.vector.tensor_tensor(out=act_grouped[:], in0=square[:], in1=factor[:], op=ALU.mult)
             act_codes = act_pool.tile([P, n_tok], U32, tag="act_codes", align_bytes=64)
             act_scales = act_pool.tile([P, n_tok], U8, tag="act_scales", align_bytes=64)
             nc.vector.quantize_mx(out=act_codes[:].bitcast(FP8X4), scales=act_scales[:], in_=act_grouped[:])
@@ -238,41 +233,30 @@ def tile_block_pc_kernel(tc, x_mid, wfc, wproj, mlp_scale, out):
                     )
                     nc.sync.dma_start(out=out_rows[tt * P : (tt + 1) * P, d_cols], in_=result[:])
 
-        chunk_tiles = [list(range(tok0 // P, (tok0 + n_tok) // P)) for tok0, n_tok in TOKEN_CHUNKS]
-        for tt in chunk_tiles[0]:
+        for tt in range(TOKEN_TILES):
             load_x(tt)
         wfc_blocks = load_wfc(0)
         wproj_blocks = load_wproj_pair(0)
-        for tt in chunk_tiles[1] + chunk_tiles[2]:
-            load_x(tt)
-        nc.gpsimd.dma_start(out=gain[:], in_=mlp_scale.partition_broadcast(P))
-        sorted_tiles = [(tt, normalise(tt)) for tt in chunk_tiles[0]]
-        for tt, h_sorted in sorted_tiles:
-            quantise_h(tt, h_sorted)
+        for tt in range(TOKEN_TILES):
+            quantise_h(tt, normalise(tt))
         quantise_weights(transpose_weights(wfc_blocks, False), wfc_codes, wfc_scales, 0)
-        quantise_weights(transpose_weights(wproj_blocks[0], True), wproj_codes, wproj_scales, 0)
+        quantise_weights(transpose_weights(wproj_blocks[0], False), wproj_codes, wproj_scales, 0)
 
         waiting = []
-        for ci, (tok0, n_tok) in enumerate(TOKEN_CHUNKS):
-            next_tiles = chunk_tiles[ci + 1] if ci + 1 < len(TOKEN_CHUNKS) else []
+        for tok0, n_tok in TOKEN_CHUNKS:
             for g in range(F_GROUPS):
-                prepare = ci == 0 and g + 1 < F_GROUPS
-                if prepare:
+                if tok0 == 0 and g + 1 < F_GROUPS:
                     wfc_stage = transpose_weights(load_wfc(g + 1), False)
                     quantise_weights(wfc_stage, wfc_codes, wfc_scales, g + 1)
                     if (g + 1) % 2 == 0:
                         wproj_blocks = load_wproj_pair(g + 1)
-                    wproj_stage = transpose_weights(wproj_blocks[(g + 1) % 2], True)
-                if g == 1:
-                    for tt, h_sorted in sorted_tiles:
-                        quantise_h(tt, h_sorted)
-                square, factor = hidden_matmul(tok0, n_tok, g)
-                if prepare:
+                    wproj_stage = transpose_weights(wproj_blocks[(g + 1) % 2], False)
                     quantise_weights(wproj_stage, wproj_codes, wproj_scales, g + 1)
-                codes_and_scales = quantise_act(n_tok, square, factor)
-                if g == 0:
-                    sorted_tiles = [(tt, normalise(tt)) for tt in next_tiles]
-                if waiting:
-                    project_group(*waiting.pop())
-                waiting.append((tok0, n_tok, g) + codes_and_scales)
-        project_group(*waiting.pop())
+                if tok0 == 0 and g + 1 == F_GROUPS:
+                    nc.sync.dma_start(out=gain[:], in_=mlp_scale.partition_broadcast(P))
+                square, factor = hidden_matmul(tok0, n_tok, g)
+                waiting.append((tok0, n_tok, g) + quantise_act(n_tok, square, factor))
+                if len(waiting) > LAG:
+                    project_group(*waiting.pop(0))
+        for args in waiting:
+            project_group(*args)

@@ -21,9 +21,9 @@ D_PASSES = D // K_PASS
 F_GROUPS = F // K_PASS
 TOKEN_TILES = T // P
 GROUP_WORDS = 1024
-TOKEN_CHUNKS = ((0, 256), (256, 256), (512, 128))
+TOKEN_CHUNKS = ((0, 256), (256, 128), (384, 128), (512, 128))
 
-LAG = 2
+LAG = 3
 
 FLOPS = 2 * 2 * T * D * F
 
@@ -39,7 +39,7 @@ def tile_block_pc_kernel(tc, x_mid, wfc, wproj, mlp_scale, out):
         wproj_pool = pools.enter_context(tc.tile_pool(name="wproj_raw", bufs=2))
         stage_pool = pools.enter_context(tc.tile_pool(name="stage", bufs=3))
         norm_pool = pools.enter_context(tc.tile_pool(name="norm", bufs=2))
-        act_pool = pools.enter_context(tc.tile_pool(name="act", bufs=4))
+        act_pool = pools.enter_context(tc.tile_pool(name="act", bufs=3))
         out_pool = pools.enter_context(tc.tile_pool(name="outp", bufs=4))
         work = pools.enter_context(tc.psum_pool(name="work", bufs=4))
         acc_pool = pools.enter_context(tc.psum_pool(name="acc", bufs=1))
@@ -191,8 +191,8 @@ def tile_block_pc_kernel(tc, x_mid, wfc, wproj, mlp_scale, out):
         def quantise_act(n_tok, square, factor):
             act_grouped = act_pool.tile([P, 4 * n_tok], BF16, tag="act_grouped", align_bytes=64)
             nc.vector.tensor_tensor(out=act_grouped[:], in0=square[:], in1=factor[:], op=ALU.mult)
-            act_codes = act_pool.tile([P, n_tok], U32, tag="act_codes", align_bytes=64)
-            act_scales = act_pool.tile([P, n_tok], U8, tag="act_scales", align_bytes=64)
+            act_codes = act_pool.tile([P, n_tok], U32, tag="act_codes", align_bytes=64, bufs=LAG + 2)
+            act_scales = act_pool.tile([P, n_tok], U8, tag="act_scales", align_bytes=64, bufs=LAG + 2)
             nc.vector.quantize_mx(out=act_codes[:].bitcast(FP8X4), scales=act_scales[:], in_=act_grouped[:])
             return act_codes, act_scales
 
@@ -200,14 +200,15 @@ def tile_block_pc_kernel(tc, x_mid, wfc, wproj, mlp_scale, out):
 
         def project_group(tok0, n_tok, g, act_codes, act_scales):
             for ti in range(n_tok // P):
+                slot = (tok0 // P + ti) % 2
                 for half in range(D // BANK):
                     if g == 0:
-                        sums[(ti, half)] = acc_pool.tile(
-                            [P, BANK], F32, name="sum_%d_%d" % (ti, half), tag="sum_%d_%d" % (ti, half)
+                        sums[(slot, half)] = acc_pool.tile(
+                            [P, BANK], F32, name="sum_%d_%d" % (slot, half), tag="sum_%d_%d" % (slot, half)
                         )
                     w_cols = slice(g * GROUP_WORDS + half * BANK, g * GROUP_WORDS + (half + 1) * BANK)
                     nc.tensor.matmul_mx(
-                        out=sums[(ti, half)][:],
+                        out=sums[(slot, half)][:],
                         lhsT=act_codes[:, ti * P : (ti + 1) * P].bitcast(FP8X4),
                         lhsT_scale=act_scales[:, ti * P : (ti + 1) * P],
                         rhs=wproj_codes[:, w_cols].bitcast(FP8X4),
@@ -219,13 +220,15 @@ def tile_block_pc_kernel(tc, x_mid, wfc, wproj, mlp_scale, out):
                 return
             for ti in range(n_tok // P):
                 tt = tok0 // P + ti
+                slot = tt % 2
                 for half in range(D // BANK):
                     d_cols = slice(half * BANK, (half + 1) * BANK)
                     result = out_pool.tile([P, BANK], F32)
                     nc.vector.tensor_tensor(
-                        out=result[:], in0=sums[(ti, half)][:], in1=gain[:, d_cols], op=ALU.mult
+                        out=result[:], in0=sums[(slot, half)][:], in1=gain[:, d_cols], op=ALU.mult
                     )
-                    nc.gpsimd.tensor_tensor(
+                    adder = nc.vector if tt == TOKEN_TILES - 1 else nc.gpsimd
+                    adder.tensor_tensor(
                         out=result[:],
                         in0=result[:],
                         in1=x_sb[:, tt * D + half * BANK : tt * D + (half + 1) * BANK],
@@ -237,7 +240,7 @@ def tile_block_pc_kernel(tc, x_mid, wfc, wproj, mlp_scale, out):
             load_x(tt)
         wfc_blocks = load_wfc(0)
         wproj_blocks = load_wproj_pair(0)
-        for tt in range(TOKEN_TILES):
+        for tt in range(TOKEN_CHUNKS[0][1] // P):
             quantise_h(tt, normalise(tt))
         quantise_weights(transpose_weights(wfc_blocks, False), wfc_codes, wfc_scales, 0)
         quantise_weights(transpose_weights(wproj_blocks[0], False), wproj_codes, wproj_scales, 0)
@@ -245,6 +248,8 @@ def tile_block_pc_kernel(tc, x_mid, wfc, wproj, mlp_scale, out):
         waiting = []
         for tok0, n_tok in TOKEN_CHUNKS:
             for g in range(F_GROUPS):
+                if g == 0 and tok0 + n_tok < T:
+                    quantise_h((tok0 + n_tok) // P, normalise((tok0 + n_tok) // P))
                 if tok0 == 0 and g + 1 < F_GROUPS:
                     wfc_stage = transpose_weights(load_wfc(g + 1), False)
                     quantise_weights(wfc_stage, wfc_codes, wfc_scales, g + 1)

@@ -21,9 +21,14 @@ D_PASSES = D // K_PASS
 F_GROUPS = F // K_PASS
 TOKEN_TILES = T // P
 GROUP_WORDS = 1024
-TOKEN_CHUNKS = ((0, 256), (256, 128), (384, 128), (512, 128))
-
-LAG = 3
+WORK_BANKS = 5
+ACC_BANKS = 3
+UNIT_LAG = 3
+UNIT_CODES = 8
+EARLY = ((0, 0), (0, 1), (1, 0))
+WFC_ENGINES = ("scalar", "scalar", "vector", "scalar")
+WPROJ_ENGINES = ("scalar", "scalar", "vector", "scalar")
+LAG = 2
 
 FLOPS = 2 * 2 * T * D * F
 
@@ -34,29 +39,21 @@ def tile_block_pc_kernel(tc, x_mid, wfc, wproj, mlp_scale, out):
     out_rows = out.flatten_outer_dims()
 
     with ExitStack() as pools:
+        pools.enter_context(tc.manual_schedule())
         keep = pools.enter_context(tc.tile_pool(name="keep", bufs=1))
-        wfc_pool = pools.enter_context(tc.tile_pool(name="wfc_raw", bufs=3))
+        wfc_pool = pools.enter_context(tc.tile_pool(name="wfc_raw", bufs=4))
         wproj_pool = pools.enter_context(tc.tile_pool(name="wproj_raw", bufs=2))
         stage_pool = pools.enter_context(tc.tile_pool(name="stage", bufs=3))
         norm_pool = pools.enter_context(tc.tile_pool(name="norm", bufs=2))
         act_pool = pools.enter_context(tc.tile_pool(name="act", bufs=3))
-        out_pool = pools.enter_context(tc.tile_pool(name="outp", bufs=4))
-        work = pools.enter_context(tc.psum_pool(name="work", bufs=4))
+        out_pool = pools.enter_context(tc.tile_pool(name="outp", bufs=3))
+        work = pools.enter_context(tc.psum_pool(name="work", bufs=WORK_BANKS))
         acc_pool = pools.enter_context(tc.psum_pool(name="acc", bufs=1))
-
-        ident_f32 = keep.tile([P, P], F32)
-        make_identity(nc, ident_f32[:])
-        ident_bf16 = keep.tile([P, P], BF16)
-        make_identity(nc, ident_bf16[:])
-        eps12 = keep.tile([P, 1], F32)
-        nc.vector.memset(eps12[:], 12.0e-6)
-        warm = keep.tile([P, 1], F32)
-        nc.scalar.activation(out=warm[:], in_=eps12[:], func=FUNC.Sqrt)
 
         x_sb = keep.tile([P, TOKEN_TILES * D], BF16)
         gain = keep.tile([P, D], BF16)
-        h_codes = keep.tile([P, D_PASSES * T], U32, align_bytes=64)
-        h_scales = keep.tile([P, D_PASSES * T], U8, align_bytes=64)
+        h_codes = keep.tile([P, TOKEN_TILES * D_PASSES * P], U32, align_bytes=64)
+        h_scales = keep.tile([P, TOKEN_TILES * D_PASSES * P], U8, align_bytes=64)
         wfc_codes = keep.tile([P, F_GROUPS * GROUP_WORDS], U32, align_bytes=64)
         wfc_scales = keep.tile([P, F_GROUPS * GROUP_WORDS], U8, align_bytes=64)
         wproj_codes = keep.tile([P, F_GROUPS * GROUP_WORDS], U32, align_bytes=64)
@@ -64,52 +61,12 @@ def tile_block_pc_kernel(tc, x_mid, wfc, wproj, mlp_scale, out):
         sumsq = keep.tile([P, TOKEN_TILES], F32)
         rms = keep.tile([P, TOKEN_TILES], F32)
         rstd = keep.tile([P, TOKEN_TILES], F32)
+        eps12 = keep.tile([P, 1], F32)
+        warm = keep.tile([P, 1], F32)
+        ident_f32 = keep.tile([P, P], F32)
 
         def load_x(tt):
             nc.sync.dma_start(out=x_sb[:, tt * D : (tt + 1) * D], in_=x_rows[tt * P : (tt + 1) * P, :])
-
-        def normalise(tt):
-            x_tile = x_sb[:, tt * D : (tt + 1) * D]
-            squares = norm_pool.tile([P, D], BF16)
-            nc.scalar.activation(
-                out=squares[:], in_=x_tile, func=FUNC.Square, accum_out=sumsq[:, tt : tt + 1]
-            )
-            nc.scalar.activation(
-                out=rms[:, tt : tt + 1],
-                in_=sumsq[:, tt : tt + 1],
-                func=FUNC.Sqrt,
-                scale=12.0 / D,
-                bias=eps12[:],
-            )
-            nc.vector.reciprocal(out=rstd[:, tt : tt + 1], in_=rms[:, tt : tt + 1])
-            h_sorted = norm_pool.tile([P, D], BF16)
-            nc.vector.tensor_scalar(
-                out=h_sorted[:].rearrange("t (b e p) -> t b e p", b=4, e=2),
-                in0=x_tile.rearrange("t (b p e) -> t b e p", b=4, e=2),
-                scalar1=rstd[:, tt : tt + 1],
-                scalar2=None,
-                op0=ALU.mult,
-            )
-            return h_sorted
-
-        def quantise_h(tt, h_sorted):
-            h_bank = work.tile([P, 2 * BANK], BF16, tag="work")
-            for blk in range(D // P):
-                nc.tensor.transpose(
-                    h_bank[:, blk * P : (blk + 1) * P], h_sorted[:, blk * P : (blk + 1) * P], ident_bf16[:]
-                )
-            h_grouped = norm_pool.tile([P, D], BF16, align_bytes=64)
-            nc.scalar.copy(
-                out=h_grouped[:].rearrange("p (c r t) -> p c r t", c=D_PASSES, t=4),
-                in_=h_bank[:].rearrange("p (c t r) -> p c r t", c=D_PASSES, t=4),
-            )
-            for c in range(D_PASSES):
-                cols = slice(c * T + tt * P, c * T + (tt + 1) * P)
-                nc.vector.quantize_mx(
-                    out=h_codes[:, cols].bitcast(FP8X4),
-                    scales=h_scales[:, cols],
-                    in_=h_grouped[:, c * K_PASS : (c + 1) * K_PASS],
-                )
 
         def load_wfc(g):
             wfc_raw = wfc_pool.tile([P, 4 * GROUP_WORDS], BF16)
@@ -132,136 +89,280 @@ def tile_block_pc_kernel(tc, x_mid, wfc, wproj, mlp_scale, out):
                 for i in range(2)
             ]
 
-        def transpose_weights(blocks, last_bank_on_vector):
-            stage = stage_pool.tile([P, 4 * GROUP_WORDS], BF16, align_bytes=64)
-            stage_words = stage[:].bitcast(F32)
-            for b in range(4):
-                bank = work.tile([P, BANK], F32, tag="work")
-                for i in range(4):
-                    nc.tensor.transpose(bank[:, i * P : (i + 1) * P], blocks[4 * b + i], ident_f32[:])
-                stage_part = stage_words[:, b * BANK : (b + 1) * BANK].rearrange(
-                    "p (r m u) -> p r m u", r=2, u=2
+        def square_sum(tt, engine):
+            x_tile = x_sb[:, tt * D : (tt + 1) * D]
+            squares = norm_pool.tile([P, D], BF16)
+            if engine == "scalar":
+                nc.scalar.activation(out=squares[:], in_=x_tile, func=FUNC.Square, accum_out=sumsq[:, tt : tt + 1])
+            else:
+                nc.vector.scalar_tensor_tensor(
+                    out=squares[:], in0=x_tile, scalar=1.0, in1=x_tile, op0=ALU.mult, op1=ALU.mult,
+                    accum_out=sumsq[:, tt : tt + 1],
                 )
-                bank_view = bank[:].rearrange("p (r u m) -> p r m u", r=2, u=2)
-                if last_bank_on_vector and b == 3:
-                    nc.vector.tensor_copy(out=stage_part, in_=bank_view)
-                else:
-                    nc.scalar.copy(out=stage_part, in_=bank_view)
+
+        def root(tt):
+            nc.scalar.activation(
+                out=rms[:, tt : tt + 1], in_=sumsq[:, tt : tt + 1], func=FUNC.Sqrt, scale=12.0 / D, bias=eps12[:]
+            )
+
+        def scale_h(tt):
+            nc.vector.reciprocal(out=rstd[:, tt : tt + 1], in_=rms[:, tt : tt + 1])
+            h_rows = norm_pool.tile([P, D], BF16)
+            nc.vector.tensor_scalar(
+                out=h_rows[:], in0=x_sb[:, tt * D : (tt + 1) * D], scalar1=rstd[:, tt : tt + 1], scalar2=None, op0=ALU.mult
+            )
+            return h_rows
+
+        def transpose_h(h_rows):
+            words = h_rows[:].bitcast(F32)
+            h_bank = work.tile([P, BANK], F32, tag="work")
+            for n in range(4):
+                nc.tensor.transpose(h_bank[:, n * P : (n + 1) * P], words[:, n * P : (n + 1) * P], ident_f32[:])
+            return h_bank
+
+        def group_h(h_bank):
+            h_grouped = norm_pool.tile([P, D], BF16, align_bytes=64)
+            nc.scalar.copy(
+                out=h_grouped[:].bitcast(F32).rearrange("p (c t u) -> p c t u", c=2, u=2),
+                in_=h_bank[:].rearrange("p (c u t) -> p c t u", c=2, u=2),
+            )
+            return h_grouped
+
+        def quantise_h(tt, h_grouped):
+            cols = slice(tt * 2 * P, (tt + 1) * 2 * P)
+            nc.vector.quantize_mx(out=h_codes[:, cols].bitcast(FP8X4), scales=h_scales[:, cols], in_=h_grouped[:])
+
+        def transpose_bank(blocks, b):
+            bank = work.tile([P, BANK], F32, tag="work")
+            for i in range(4):
+                nc.tensor.transpose(bank[:, i * P : (i + 1) * P], blocks[4 * b + i], ident_f32[:])
+            return bank
+
+        def copy_bank(stage, b, bank, engine):
+            stage_part = stage[:].bitcast(F32)[:, b * BANK : (b + 1) * BANK].rearrange("p (r m u) -> p r m u", r=2, u=2)
+            bank_view = bank[:].rearrange("p (r u m) -> p r m u", r=2, u=2)
+            if engine == "scalar":
+                nc.scalar.copy(out=stage_part, in_=bank_view)
+            else:
+                nc.vector.tensor_copy(out=stage_part, in_=bank_view)
+
+        def transpose_weights(blocks, engines):
+            stage = stage_pool.tile([P, 4 * GROUP_WORDS], BF16, align_bytes=64)
+            banks = [transpose_bank(blocks, b) for b in range(4)]
+            for b in range(4):
+                copy_bank(stage, b, banks[b], engines[b])
             return stage
 
         def quantise_weights(stage, codes, scales, g):
             group = slice(g * GROUP_WORDS, (g + 1) * GROUP_WORDS)
             nc.vector.quantize_mx(out=codes[:, group].bitcast(FP8X4), scales=scales[:, group], in_=stage[:])
 
-        def hidden_matmul(tok0, n_tok, g):
-            square = act_pool.tile([P, 4 * n_tok], BF16, tag="square")
-            factor = act_pool.tile([P, 4 * n_tok], BF16, tag="factor")
-            for ti in range(n_tok // P):
-                u_bank = work.tile([P, BANK], F32, tag="work")
-                for j in range(4):
-                    for c in range(D_PASSES):
-                        w_cols = slice(
-                            g * GROUP_WORDS + (2 * j + c) * P, g * GROUP_WORDS + (2 * j + c + 1) * P
-                        )
-                        h_cols = slice(c * T + tok0 + ti * P, c * T + tok0 + (ti + 1) * P)
-                        nc.tensor.matmul_mx(
-                            out=u_bank[:, j * P : (j + 1) * P],
-                            lhsT=wfc_codes[:, w_cols].bitcast(FP8X4),
-                            lhsT_scale=wfc_scales[:, w_cols],
-                            rhs=h_codes[:, h_cols].bitcast(FP8X4),
-                            rhs_scale=h_scales[:, h_cols],
-                            start=(c == 0),
-                            stop=(c == D_PASSES - 1),
-                        )
-                part = slice(ti * BANK, (ti + 1) * BANK)
-                words = u_bank[:].rearrange("p (j t) -> p t j", j=4)
-                nc.scalar.activation(
-                    out=square[:, part].rearrange("p (t j) -> p t j", j=4), in_=words, func=FUNC.Square
-                )
-                nc.vector.tensor_scalar(
-                    out=factor[:, part].rearrange("p (t j) -> p t j", j=4),
-                    in0=words,
-                    scalar1=0.0,
-                    scalar2=0.25,
-                    op0=ALU.is_ge,
-                    op1=ALU.max,
-                )
-            return square, factor
+        def hidden_matmul(tt, g):
+            u_bank = work.tile([P, BANK], F32, tag="work")
+            for j in range(4):
+                for c in range(D_PASSES):
+                    w_cols = slice(g * GROUP_WORDS + (2 * j + c) * P, g * GROUP_WORDS + (2 * j + c + 1) * P)
+                    h_cols = slice((2 * tt + c) * P, (2 * tt + c + 1) * P)
+                    nc.tensor.matmul_mx(
+                        out=u_bank[:, j * P : (j + 1) * P],
+                        lhsT=wfc_codes[:, w_cols].bitcast(FP8X4),
+                        lhsT_scale=wfc_scales[:, w_cols],
+                        rhs=h_codes[:, h_cols].bitcast(FP8X4),
+                        rhs_scale=h_scales[:, h_cols],
+                        start=(c == 0),
+                        stop=(c == D_PASSES - 1),
+                    )
+            return u_bank
 
-        def quantise_act(n_tok, square, factor):
-            act_grouped = act_pool.tile([P, 4 * n_tok], BF16, tag="act_grouped", align_bytes=64)
-            nc.vector.tensor_tensor(out=act_grouped[:], in0=square[:], in1=factor[:], op=ALU.mult)
-            act_codes = act_pool.tile([P, n_tok], U32, tag="act_codes", align_bytes=64, bufs=LAG + 2)
-            act_scales = act_pool.tile([P, n_tok], U8, tag="act_scales", align_bytes=64, bufs=LAG + 2)
+        def evacuate(u_bank, square, factor, ti, engine):
+            part = slice(ti * BANK, (ti + 1) * BANK)
+            words = u_bank[:].rearrange("p (j t) -> p t j", j=4)
+            nc.scalar.activation(out=square[:, part].rearrange("p (t j) -> p t j", j=4), in_=words, func=FUNC.Square)
+            factor_part = factor[:, part].rearrange("p (t j) -> p t j", j=4)
+            if engine == "scalar":
+                nc.scalar.activation(out=factor_part, in_=words, func=FUNC.Sign)
+            else:
+                nc.vector.tensor_scalar(out=factor_part, in0=words, scalar1=0.0, scalar2=0.25, op0=ALU.is_ge, op1=ALU.max)
+
+        def multiply(n, square, factor, engine):
+            act_grouped = act_pool.tile([P, n * BANK], BF16, tag="act_grouped", align_bytes=64)
+            if engine == "scalar":
+                nc.vector.scalar_tensor_tensor(
+                    out=act_grouped[:], in0=factor[:], scalar=0.25, in1=square[:], op0=ALU.max, op1=ALU.mult
+                )
+            else:
+                nc.vector.tensor_tensor(out=act_grouped[:], in0=square[:], in1=factor[:], op=ALU.mult)
+            return act_grouped
+
+        def quantise_act(n, act_grouped):
+            bufs = F_GROUPS if n == 2 else UNIT_CODES
+            act_codes = act_pool.tile([P, n * P], U32, tag="act_codes_%d" % n, align_bytes=64, bufs=bufs)
+            act_scales = act_pool.tile([P, n * P], U8, tag="act_scales_%d" % n, align_bytes=64, bufs=bufs)
             nc.vector.quantize_mx(out=act_codes[:].bitcast(FP8X4), scales=act_scales[:], in_=act_grouped[:])
             return act_codes, act_scales
 
         sums = {}
 
-        def project_group(tok0, n_tok, g, act_codes, act_scales):
-            for ti in range(n_tok // P):
-                slot = (tok0 // P + ti) % 2
-                for half in range(D // BANK):
-                    if g == 0:
-                        sums[(slot, half)] = acc_pool.tile(
-                            [P, BANK], F32, name="sum_%d_%d" % (slot, half), tag="sum_%d_%d" % (slot, half)
-                        )
-                    w_cols = slice(g * GROUP_WORDS + half * BANK, g * GROUP_WORDS + (half + 1) * BANK)
-                    nc.tensor.matmul_mx(
-                        out=sums[(slot, half)][:],
-                        lhsT=act_codes[:, ti * P : (ti + 1) * P].bitcast(FP8X4),
-                        lhsT_scale=act_scales[:, ti * P : (ti + 1) * P],
-                        rhs=wproj_codes[:, w_cols].bitcast(FP8X4),
-                        rhs_scale=wproj_scales[:, w_cols],
-                        start=(g == 0),
-                        stop=(g == F_GROUPS - 1),
-                    )
-            if g < F_GROUPS - 1:
-                return
-            for ti in range(n_tok // P):
-                tt = tok0 // P + ti
-                slot = tt % 2
-                for half in range(D // BANK):
-                    d_cols = slice(half * BANK, (half + 1) * BANK)
-                    result = out_pool.tile([P, BANK], F32)
-                    nc.vector.tensor_tensor(
-                        out=result[:], in0=sums[(slot, half)][:], in1=gain[:, d_cols], op=ALU.mult
-                    )
-                    adder = nc.vector if tt == TOKEN_TILES - 1 else nc.gpsimd
-                    adder.tensor_tensor(
-                        out=result[:],
-                        in0=result[:],
-                        in1=x_sb[:, tt * D + half * BANK : tt * D + (half + 1) * BANK],
-                        op=ALU.add,
-                    )
-                    nc.sync.dma_start(out=out_rows[tt * P : (tt + 1) * P, d_cols], in_=result[:])
+        def project(tt, half, g, act):
+            act_codes, act_scales, ti, born = act
+            ring = (2 * tt + half) % ACC_BANKS
+            if g == 0:
+                sums[(tt, half)] = acc_pool.tile([P, BANK], F32, name="sum_%d" % ring, tag="sum_%d" % ring)
+            w_cols = slice(g * GROUP_WORDS + half * BANK, g * GROUP_WORDS + (half + 1) * BANK)
+            nc.tensor.matmul_mx(
+                out=sums[(tt, half)][:],
+                lhsT=act_codes[:, ti * P : (ti + 1) * P].bitcast(FP8X4),
+                lhsT_scale=act_scales[:, ti * P : (ti + 1) * P],
+                rhs=wproj_codes[:, w_cols].bitcast(FP8X4),
+                rhs_scale=wproj_scales[:, w_cols],
+                start=(g == 0),
+                stop=(g == F_GROUPS - 1),
+            )
 
-        for tt in range(TOKEN_TILES):
-            load_x(tt)
-        wfc_blocks = load_wfc(0)
-        wproj_blocks = load_wproj_pair(0)
-        for tt in range(TOKEN_CHUNKS[0][1] // P):
-            quantise_h(tt, normalise(tt))
-        quantise_weights(transpose_weights(wfc_blocks, False), wfc_codes, wfc_scales, 0)
-        quantise_weights(transpose_weights(wproj_blocks[0], False), wproj_codes, wproj_scales, 0)
+        def finish(tt, half):
+            d_cols = slice(half * BANK, (half + 1) * BANK)
+            result = out_pool.tile([P, BANK], F32)
+            nc.vector.tensor_tensor(out=result[:], in0=sums[(tt, half)][:], in1=gain[:, d_cols], op=ALU.mult)
+            adder = nc.vector if tt == TOKEN_TILES - 1 else nc.gpsimd
+            adder.tensor_tensor(
+                out=result[:], in0=result[:], in1=x_sb[:, tt * D + half * BANK : tt * D + (half + 1) * BANK], op=ALU.add
+            )
+            nc.sync.dma_start(out=out_rows[tt * P : (tt + 1) * P, d_cols], in_=result[:])
 
-        waiting = []
-        for tok0, n_tok in TOKEN_CHUNKS:
-            for g in range(F_GROUPS):
-                if g == 0 and tok0 + n_tok < T:
-                    quantise_h((tok0 + n_tok) // P, normalise((tok0 + n_tok) // P))
-                if tok0 == 0 and g + 1 < F_GROUPS:
-                    wfc_stage = transpose_weights(load_wfc(g + 1), False)
-                    quantise_weights(wfc_stage, wfc_codes, wfc_scales, g + 1)
-                    if (g + 1) % 2 == 0:
-                        wproj_blocks = load_wproj_pair(g + 1)
-                    wproj_stage = transpose_weights(wproj_blocks[(g + 1) % 2], False)
-                    quantise_weights(wproj_stage, wproj_codes, wproj_scales, g + 1)
-                if tok0 == 0 and g + 1 == F_GROUPS:
-                    nc.sync.dma_start(out=gain[:], in_=mlp_scale.partition_broadcast(P))
-                square, factor = hidden_matmul(tok0, n_tok, g)
-                waiting.append((tok0, n_tok, g) + quantise_act(n_tok, square, factor))
-                if len(waiting) > LAG:
-                    project_group(*waiting.pop(0))
-        for args in waiting:
-            project_group(*args)
+        make_identity(nc, ident_f32[:])
+        nc.vector.memset(eps12[:], 12.0e-6)
+        nc.scalar.activation(out=warm[:], in_=eps12[:], func=FUNC.Sqrt)
+        wfc_blocks = {}
+        wproj_blocks = {}
+
+        def load_pair(g):
+            wproj_blocks[g], wproj_blocks[g + 1] = load_wproj_pair(g)
+
+        load_x(0)
+        load_x(1)
+        wfc_blocks[0] = load_wfc(0)
+        wfc_blocks[1] = load_wfc(1)
+        wfc_blocks[2] = load_wfc(2)
+        load_pair(0)
+        wfc_blocks[3] = load_wfc(3)
+        load_pair(2)
+        square_sum(0, "scalar")
+        square_sum(1, "vector")
+        root(0)
+        h_rows0 = scale_h(0)
+        root(1)
+        h_rows1 = scale_h(1)
+        bank0 = transpose_h(h_rows0)
+        h0 = group_h(bank0)
+        bank1 = transpose_h(h_rows1)
+        h1 = group_h(bank1)
+        stage = transpose_weights(wfc_blocks[0], ("scalar", "vector", "scalar", "vector"))
+        quantise_h(0, h0)
+        quantise_h(1, h1)
+        quantise_weights(stage, wfc_codes, wfc_scales, 0)
+
+        acts = {}
+        pending = None
+        done = {}
+
+        def project_ready(tt, half, upto):
+            g = done.get((tt, half), 0)
+            while g <= upto and (tt, g) in acts:
+                project(tt, half, g, acts[(tt, g)])
+                g += 1
+            done[(tt, half)] = g
+
+        for g in range(F_GROUPS):
+            wf = g + 1
+            wp = g - 1
+            if wf < F_GROUPS:
+                if wf + 3 < F_GROUPS:
+                    wfc_blocks[wf + 3] = load_wfc(wf + 3)
+                stage = transpose_weights(wfc_blocks[wf], WFC_ENGINES)
+            if pending is not None:
+                act_grouped = multiply(2, pending[1], pending[2], "vector")
+            if wf < F_GROUPS:
+                quantise_weights(stage, wfc_codes, wfc_scales, wf)
+            for tt, half in EARLY:
+                project_ready(tt, half, g - 3)
+            if pending is not None:
+                codes, scales = quantise_act(2, act_grouped)
+                acts[(0, pending[0])] = (codes, scales, 0, 0)
+                acts[(1, pending[0])] = (codes, scales, 1, 0)
+            if wp >= 0:
+                stage = transpose_weights(wproj_blocks[wp], WPROJ_ENGINES)
+                if wp in (1, 3):
+                    load_pair(wp + 3)
+            square = act_pool.tile([P, 2 * BANK], BF16, tag="square")
+            factor = act_pool.tile([P, 2 * BANK], BF16, tag="factor")
+            banks = [hidden_matmul(tt, g) for tt in range(2)]
+            for ti in range(2):
+                evacuate(banks[ti], square, factor, ti, "vector")
+            if wp >= 0:
+                quantise_weights(stage, wproj_codes, wproj_scales, wp)
+            pending = (g, square, factor)
+            if g == 3:
+                for tt in range(2, TOKEN_TILES):
+                    load_x(tt)
+            if g == 4:
+                nc.sync.dma_start(out=gain[:], in_=mlp_scale.partition_broadcast(P))
+            if g == 5:
+                square_sum(2, "scalar")
+                root(2)
+            if g == 6:
+                h_rows = scale_h(2)
+                h1 = group_h(transpose_h(h_rows))
+                quantise_h(2, h1)
+
+        units = [(tt, g) for tt in range(2, TOKEN_TILES) for g in range(F_GROUPS)]
+        todo = []
+        for tt, half in EARLY:
+            todo += [(tt, half, g) for g in range(done[(tt, half)], F_GROUPS)]
+        todo.sort(key=lambda k: (k[2], k[0], k[1]))
+        for half in range(2):
+            if (1, half) not in EARLY:
+                todo += [(1, half, g) for g in range(F_GROUPS)]
+        todo += [(tt, half, g) for tt in range(2, TOKEN_TILES) for g in range(F_GROUPS) for half in range(2)]
+
+        def some_projects(n, age):
+            while n > 0 and todo and (todo[0][0], todo[0][2]) in acts and acts[(todo[0][0], todo[0][2])][3] <= age:
+                tt, half, g = todo.pop(0)
+                project(tt, half, g, acts[(tt, g)])
+                n -= 1
+                if g == F_GROUPS - 1:
+                    finish(tt, half)
+
+        pending = (0, 2, F_GROUPS - 1, square, factor, "vector")
+        h_at = {}
+        for n, (tt, g) in enumerate(units):
+            if n == 0:
+                stage = transpose_weights(wproj_blocks[F_GROUPS - 1], WPROJ_ENGINES)
+            u_bank = hidden_matmul(tt, g)
+            engine = "scalar" if g % 2 == 1 else "vector"
+            square = act_pool.tile([P, BANK], BF16, tag="square")
+            factor = act_pool.tile([P, BANK], BF16, tag="factor")
+            evacuate(u_bank, square, factor, 0, engine)
+            t0, nt, g0, sq0, fa0, en0 = pending
+            act_grouped = multiply(nt, sq0, fa0, en0)
+            if n == 0:
+                quantise_weights(stage, wproj_codes, wproj_scales, F_GROUPS - 1)
+            if tt + 1 < TOKEN_TILES:
+                if g == 0:
+                    square_sum(tt + 1, "scalar")
+                if g == 1:
+                    root(tt + 1)
+                if g == 2:
+                    h_rows = scale_h(tt + 1)
+                if g == 5:
+                    h1 = group_h(transpose_h(h_rows))
+                if g == 6:
+                    quantise_h(tt + 1, h1)
+            codes, scales = quantise_act(nt, act_grouped)
+            for ti in range(nt):
+                acts[(t0 + ti, g0)] = (codes, scales, ti, n)
+            some_projects(-(-(len(todo) - 2 * UNIT_LAG) // (len(units) - n)), n - UNIT_LAG)
+            pending = (tt, 1, g, square, factor, engine)
+        t0, nt, g0, sq0, fa0, en0 = pending
+        codes, scales = quantise_act(nt, multiply(nt, sq0, fa0, en0))
+        acts[(t0, g0)] = (codes, scales, 0, 0)
+        some_projects(1000, 1000)

@@ -24,7 +24,11 @@ GROUP_WORDS = 1024
 WORK_BANKS = 5
 ACC_BANKS = 3
 UNIT_LAG = 3
-UNIT_CODES = 8
+PAIR_ENGINES = ("vector", "scalar")
+ADDER = "gpsimd"
+UNIT_ENGINES = ("scalar",)
+H_STEPS = (0, 1, 2, 5, 6)
+UNIT_CODES = 10
 EARLY = ((0, 0), (0, 1), (1, 0))
 WFC_ENGINES = ("scalar", "scalar", "vector", "scalar")
 WPROJ_ENGINES = ("scalar", "scalar", "vector", "scalar")
@@ -39,7 +43,7 @@ def tile_block_pc_kernel(tc, x_mid, wfc, wproj, mlp_scale, out):
     out_rows = out.flatten_outer_dims()
 
     with ExitStack() as pools:
-        pools.enter_context(tc.manual_schedule())
+        pools.enter_context(tc.manual_schedule(engines={mybir.EngineType.PE}))
         keep = pools.enter_context(tc.tile_pool(name="keep", bufs=1))
         wfc_pool = pools.enter_context(tc.tile_pool(name="wfc_raw", bufs=4))
         wproj_pool = pools.enter_context(tc.tile_pool(name="wproj_raw", bufs=2))
@@ -186,12 +190,13 @@ def tile_block_pc_kernel(tc, x_mid, wfc, wproj, mlp_scale, out):
 
         def multiply(n, square, factor, engine):
             act_grouped = act_pool.tile([P, n * BANK], BF16, tag="act_grouped", align_bytes=64)
-            if engine == "scalar":
-                nc.vector.scalar_tensor_tensor(
-                    out=act_grouped[:], in0=factor[:], scalar=0.25, in1=square[:], op0=ALU.max, op1=ALU.mult
-                )
-            else:
-                nc.vector.tensor_tensor(out=act_grouped[:], in0=square[:], in1=factor[:], op=ALU.mult)
+            for ti in range(n):
+                if engine[ti] == "scalar":
+                    part = slice(ti * BANK, (ti + 1) * BANK)
+                    nc.vector.tensor_scalar(
+                        out=factor[:, part], in0=factor[:, part], scalar1=0.25, scalar2=None, op0=ALU.max
+                    )
+            nc.vector.tensor_tensor(out=act_grouped[:], in0=square[:], in1=factor[:], op=ALU.mult)
             return act_grouped
 
         def quantise_act(n, act_grouped):
@@ -223,7 +228,7 @@ def tile_block_pc_kernel(tc, x_mid, wfc, wproj, mlp_scale, out):
             d_cols = slice(half * BANK, (half + 1) * BANK)
             result = out_pool.tile([P, BANK], F32)
             nc.vector.tensor_tensor(out=result[:], in0=sums[(tt, half)][:], in1=gain[:, d_cols], op=ALU.mult)
-            adder = nc.vector if tt == TOKEN_TILES - 1 else nc.gpsimd
+            adder = nc.vector if ADDER == "vector" or tt == TOKEN_TILES - 1 else nc.gpsimd
             adder.tensor_tensor(
                 out=result[:], in0=result[:], in1=x_sb[:, tt * D + half * BANK : tt * D + (half + 1) * BANK], op=ALU.add
             )
@@ -245,7 +250,6 @@ def tile_block_pc_kernel(tc, x_mid, wfc, wproj, mlp_scale, out):
         wfc_blocks[2] = load_wfc(2)
         load_pair(0)
         wfc_blocks[3] = load_wfc(3)
-        load_pair(2)
         square_sum(0, "scalar")
         square_sum(1, "vector")
         root(0)
@@ -278,9 +282,11 @@ def tile_block_pc_kernel(tc, x_mid, wfc, wproj, mlp_scale, out):
             if wf < F_GROUPS:
                 if wf + 3 < F_GROUPS:
                     wfc_blocks[wf + 3] = load_wfc(wf + 3)
+                if wf == 1:
+                    load_pair(2)
                 stage = transpose_weights(wfc_blocks[wf], WFC_ENGINES)
             if pending is not None:
-                act_grouped = multiply(2, pending[1], pending[2], "vector")
+                act_grouped = multiply(2, pending[1], pending[2], PAIR_ENGINES)
             if wf < F_GROUPS:
                 quantise_weights(stage, wfc_codes, wfc_scales, wf)
             for tt, half in EARLY:
@@ -297,7 +303,7 @@ def tile_block_pc_kernel(tc, x_mid, wfc, wproj, mlp_scale, out):
             factor = act_pool.tile([P, 2 * BANK], BF16, tag="factor")
             banks = [hidden_matmul(tt, g) for tt in range(2)]
             for ti in range(2):
-                evacuate(banks[ti], square, factor, ti, "vector")
+                evacuate(banks[ti], square, factor, ti, PAIR_ENGINES[ti])
             if wp >= 0:
                 quantise_weights(stage, wproj_codes, wproj_scales, wp)
             pending = (g, square, factor)
@@ -306,12 +312,14 @@ def tile_block_pc_kernel(tc, x_mid, wfc, wproj, mlp_scale, out):
                     load_x(tt)
             if g == 4:
                 nc.sync.dma_start(out=gain[:], in_=mlp_scale.partition_broadcast(P))
-            if g == 5:
+            if g == 4:
                 square_sum(2, "scalar")
                 root(2)
-            if g == 6:
+            if g == 5:
                 h_rows = scale_h(2)
+            if g == 6:
                 h1 = group_h(transpose_h(h_rows))
+            if g == 7:
                 quantise_h(2, h1)
 
         units = [(tt, g) for tt in range(2, TOKEN_TILES) for g in range(F_GROUPS)]
@@ -332,13 +340,13 @@ def tile_block_pc_kernel(tc, x_mid, wfc, wproj, mlp_scale, out):
                 if g == F_GROUPS - 1:
                     finish(tt, half)
 
-        pending = (0, 2, F_GROUPS - 1, square, factor, "vector")
+        pending = (0, 2, F_GROUPS - 1, square, factor, PAIR_ENGINES)
         h_at = {}
         for n, (tt, g) in enumerate(units):
             if n == 0:
                 stage = transpose_weights(wproj_blocks[F_GROUPS - 1], WPROJ_ENGINES)
             u_bank = hidden_matmul(tt, g)
-            engine = "scalar" if g % 2 == 1 else "vector"
+            engine = UNIT_ENGINES[n % len(UNIT_ENGINES)]
             square = act_pool.tile([P, BANK], BF16, tag="square")
             factor = act_pool.tile([P, BANK], BF16, tag="factor")
             evacuate(u_bank, square, factor, 0, engine)
@@ -347,21 +355,21 @@ def tile_block_pc_kernel(tc, x_mid, wfc, wproj, mlp_scale, out):
             if n == 0:
                 quantise_weights(stage, wproj_codes, wproj_scales, F_GROUPS - 1)
             if tt + 1 < TOKEN_TILES:
-                if g == 0:
+                if g == H_STEPS[0]:
                     square_sum(tt + 1, "scalar")
-                if g == 1:
+                if g == H_STEPS[1]:
                     root(tt + 1)
-                if g == 2:
+                if g == H_STEPS[2]:
                     h_rows = scale_h(tt + 1)
-                if g == 5:
+                if g == H_STEPS[3]:
                     h1 = group_h(transpose_h(h_rows))
-                if g == 6:
+                if g == H_STEPS[4]:
                     quantise_h(tt + 1, h1)
             codes, scales = quantise_act(nt, act_grouped)
             for ti in range(nt):
                 acts[(t0 + ti, g0)] = (codes, scales, ti, n)
             some_projects(-(-(len(todo) - 2 * UNIT_LAG) // (len(units) - n)), n - UNIT_LAG)
-            pending = (tt, 1, g, square, factor, engine)
+            pending = (tt, 1, g, square, factor, (engine,))
         t0, nt, g0, sq0, fa0, en0 = pending
         codes, scales = quantise_act(nt, multiply(nt, sq0, fa0, en0))
         acts[(t0, g0)] = (codes, scales, 0, 0)

@@ -28,7 +28,7 @@ PAIR_ENGINES = ("vector", "scalar")
 ADDER = "gpsimd"
 UNIT_ENGINES = ("scalar",)
 H_STEPS = (0, 1, 2, 5, 6)
-UNIT_CODES = 10
+UNIT_CODES = 9
 EARLY = ((0, 0), (0, 1), (1, 0))
 WFC_ENGINES = ("scalar", "scalar", "vector", "scalar")
 WPROJ_ENGINES = ("scalar", "scalar", "vector", "scalar")
@@ -95,7 +95,7 @@ def tile_block_pc_kernel(tc, x_mid, wfc, wproj, mlp_scale, out):
 
         def square_sum(tt, engine):
             x_tile = x_sb[:, tt * D : (tt + 1) * D]
-            squares = norm_pool.tile([P, D], BF16)
+            squares = norm_pool.tile([P, D], BF16, bufs=1)
             if engine == "scalar":
                 nc.scalar.activation(out=squares[:], in_=x_tile, func=FUNC.Square, accum_out=sumsq[:, tt : tt + 1])
             else:
@@ -234,8 +234,17 @@ def tile_block_pc_kernel(tc, x_mid, wfc, wproj, mlp_scale, out):
             )
             nc.sync.dma_start(out=out_rows[tt * P : (tt + 1) * P, d_cols], in_=result[:])
 
+        idle = keep.tile([P, BANK], BF16)
+        nc.gpsimd.memset(idle[:], 0.0)
+
+        def keep_warm(n):
+            bank = work.tile([P, BANK], F32, tag="work")
+            for i in range(n):
+                nc.tensor.matmul(bank[:], lhsT=idle[:, 0:P], rhs=idle[:], start=True, stop=True)
+
         make_identity(nc, ident_f32[:])
         nc.vector.memset(eps12[:], 12.0e-6)
+        keep_warm(8)
         nc.scalar.activation(out=warm[:], in_=eps12[:], func=FUNC.Sqrt)
         wfc_blocks = {}
         wproj_blocks = {}
@@ -261,6 +270,7 @@ def tile_block_pc_kernel(tc, x_mid, wfc, wproj, mlp_scale, out):
         bank1 = transpose_h(h_rows1)
         h1 = group_h(bank1)
         stage = transpose_weights(wfc_blocks[0], ("scalar", "vector", "scalar", "vector"))
+        keep_warm(3)
         quantise_h(0, h0)
         quantise_h(1, h1)
         quantise_weights(stage, wfc_codes, wfc_scales, 0)
@@ -291,6 +301,8 @@ def tile_block_pc_kernel(tc, x_mid, wfc, wproj, mlp_scale, out):
                 quantise_weights(stage, wfc_codes, wfc_scales, wf)
             for tt, half in EARLY:
                 project_ready(tt, half, g - 3)
+            if g < 3:
+                keep_warm(3)
             if pending is not None:
                 codes, scales = quantise_act(2, act_grouped)
                 acts[(0, pending[0])] = (codes, scales, 0, 0)

@@ -21,18 +21,23 @@ D_PASSES = D // K_PASS
 F_GROUPS = F // K_PASS
 TOKEN_TILES = T // P
 GROUP_WORDS = 1024
-WORK_BANKS = 5
 ACC_BANKS = 3
-UNIT_LAG = 3
-PAIR_ENGINES = ("vector", "scalar")
-ADDER = "gpsimd"
-UNIT_ENGINES = ("scalar",)
-H_STEPS = (0, 1, 2, 5, 6)
-UNIT_CODES = 9
+PAIR_CODES = 12
+RAW_BUFS = 7
+WARM = (8, 2)
+FIRST_0 = False
+FIRST_1 = True
+X_AFTER = 10
+FIRST_PROJECT = 3
+EARLY_PROJECTS = (2, 1)
 EARLY = ((0, 0), (0, 1), (1, 0))
 WFC_ENGINES = ("scalar", "scalar", "vector", "scalar")
 WPROJ_ENGINES = ("scalar", "scalar", "vector", "scalar")
-LAG = 2
+FACTOR_1 = ("vector", "scalar")
+FACTOR_2 = ("scalar", "scalar")
+FACTOR_3 = "scalar"
+TAIL = 6
+H_AT = ((2, (4, 4, 5, 6, 7)), (3, (5, 5, 6, 6, 7)), (4, (9, 9, 10, 12, 13)))
 
 FLOPS = 2 * 2 * T * D * F
 
@@ -45,14 +50,20 @@ def tile_block_pc_kernel(tc, x_mid, wfc, wproj, mlp_scale, out):
     with ExitStack() as pools:
         pools.enter_context(tc.manual_schedule(engines={mybir.EngineType.PE}))
         keep = pools.enter_context(tc.tile_pool(name="keep", bufs=1))
-        wfc_pool = pools.enter_context(tc.tile_pool(name="wfc_raw", bufs=4))
-        wproj_pool = pools.enter_context(tc.tile_pool(name="wproj_raw", bufs=2))
+        raw_pool = pools.enter_context(tc.tile_pool(name="raw", bufs=RAW_BUFS))
         stage_pool = pools.enter_context(tc.tile_pool(name="stage", bufs=3))
         norm_pool = pools.enter_context(tc.tile_pool(name="norm", bufs=2))
         act_pool = pools.enter_context(tc.tile_pool(name="act", bufs=3))
         out_pool = pools.enter_context(tc.tile_pool(name="outp", bufs=3))
-        work = pools.enter_context(tc.psum_pool(name="work", bufs=WORK_BANKS))
-        acc_pool = pools.enter_context(tc.psum_pool(name="acc", bufs=1))
+        psum = pools.enter_context(tc.psum_pool(name="psum", bufs=1))
+        work_banks = list(range(8))
+
+        def new_bank():
+            i = work_banks.pop(0)
+            work_banks.append(i)
+            bank = psum.tile([P, BANK], F32, name="bank_%d" % i, tag="bank_%d" % i)
+            return bank
+
 
         x_sb = keep.tile([P, TOKEN_TILES * D], BF16)
         gain = keep.tile([P, D], BF16)
@@ -72,30 +83,29 @@ def tile_block_pc_kernel(tc, x_mid, wfc, wproj, mlp_scale, out):
         def load_x(tt):
             nc.sync.dma_start(out=x_sb[:, tt * D : (tt + 1) * D], in_=x_rows[tt * P : (tt + 1) * P, :])
 
-        def load_wfc(g):
-            wfc_raw = wfc_pool.tile([P, 4 * GROUP_WORDS], BF16)
-            nc.sync.dma_start(
-                out=wfc_raw[:].rearrange("p (u x) -> p u x", u=2),
-                in_=wfc[g * K_PASS : (g + 1) * K_PASS, :].rearrange("(u p e) d -> p u (e d)", u=2, e=2),
-            )
-            words = wfc_raw[:].bitcast(F32)
+        def words_of(raw):
+            words = raw[:].bitcast(F32)
             return [words[:, n * P : (n + 1) * P] for n in range(16)]
 
-        def load_wproj_pair(g):
-            wproj_raw = wproj_pool.tile([P, 8 * GROUP_WORDS], BF16)
-            nc.sync.dma_start(
-                out=wproj_raw[:].rearrange("p (r k) -> p r k", k=2 * K_PASS),
-                in_=wproj[:, g * K_PASS : (g + 2) * K_PASS].rearrange("(r p) k -> p r k", p=P),
-            )
-            words = wproj_raw[:].bitcast(F32)
-            return [
-                [words[:, (4 * r + 2 * i + u) * P : (4 * r + 2 * i + u + 1) * P] for r in range(8) for u in range(2)]
-                for i in range(2)
-            ]
+        def load_weights(kind, g):
+            raw = raw_pool.tile([P, 4 * GROUP_WORDS], BF16, tag="raw")
+            if kind == "wfc":
+                halves = [slice(0, 2)] if g > 0 else [slice(0, 1), slice(1, 2)]
+                for u in halves:
+                    nc.sync.dma_start(
+                        out=raw[:].rearrange("p (u x) -> p u x", u=2)[:, u, :],
+                        in_=wfc[g * K_PASS : (g + 1) * K_PASS, :].rearrange("(u p e) d -> p u (e d)", u=2, e=2)[:, u, :],
+                    )
+            else:
+                nc.sync.dma_start(
+                    out=raw[:].rearrange("p (r k) -> p r k", k=K_PASS),
+                    in_=wproj[:, g * K_PASS : (g + 1) * K_PASS].rearrange("(r p) k -> p r k", p=P),
+                )
+            return words_of(raw)
 
         def square_sum(tt, engine):
             x_tile = x_sb[:, tt * D : (tt + 1) * D]
-            squares = norm_pool.tile([P, D], BF16, bufs=1)
+            squares = norm_pool.tile([P, D], BF16)
             if engine == "scalar":
                 nc.scalar.activation(out=squares[:], in_=x_tile, func=FUNC.Square, accum_out=sumsq[:, tt : tt + 1])
             else:
@@ -119,7 +129,7 @@ def tile_block_pc_kernel(tc, x_mid, wfc, wproj, mlp_scale, out):
 
         def transpose_h(h_rows):
             words = h_rows[:].bitcast(F32)
-            h_bank = work.tile([P, BANK], F32, tag="work")
+            h_bank = new_bank()
             for n in range(4):
                 nc.tensor.transpose(h_bank[:, n * P : (n + 1) * P], words[:, n * P : (n + 1) * P], ident_f32[:])
             return h_bank
@@ -132,12 +142,23 @@ def tile_block_pc_kernel(tc, x_mid, wfc, wproj, mlp_scale, out):
             )
             return h_grouped
 
+        def h_base(tt):
+            return (tt // 2) * 2 * D_PASSES * P + (tt % 2) * P
+
+        def h_step(tt):
+            return 2 * P if tt < 4 else P
+
         def quantise_h(tt, h_grouped):
-            cols = slice(tt * 2 * P, (tt + 1) * 2 * P)
-            nc.vector.quantize_mx(out=h_codes[:, cols].bitcast(FP8X4), scales=h_scales[:, cols], in_=h_grouped[:])
+            for c in range(D_PASSES):
+                cols = slice(h_base(tt) + c * h_step(tt), h_base(tt) + c * h_step(tt) + P)
+                nc.vector.quantize_mx(
+                    out=h_codes[:, cols].bitcast(FP8X4),
+                    scales=h_scales[:, cols],
+                    in_=h_grouped[:, c * K_PASS : (c + 1) * K_PASS],
+                )
 
         def transpose_bank(blocks, b):
-            bank = work.tile([P, BANK], F32, tag="work")
+            bank = new_bank()
             for i in range(4):
                 nc.tensor.transpose(bank[:, i * P : (i + 1) * P], blocks[4 * b + i], ident_f32[:])
             return bank
@@ -151,7 +172,7 @@ def tile_block_pc_kernel(tc, x_mid, wfc, wproj, mlp_scale, out):
                 nc.vector.tensor_copy(out=stage_part, in_=bank_view)
 
         def transpose_weights(blocks, engines):
-            stage = stage_pool.tile([P, 4 * GROUP_WORDS], BF16, align_bytes=64)
+            stage = stage_pool.tile([P, 4 * GROUP_WORDS], BF16, tag="stage", align_bytes=64)
             banks = [transpose_bank(blocks, b) for b in range(4)]
             for b in range(4):
                 copy_bank(stage, b, banks[b], engines[b])
@@ -161,58 +182,90 @@ def tile_block_pc_kernel(tc, x_mid, wfc, wproj, mlp_scale, out):
             group = slice(g * GROUP_WORDS, (g + 1) * GROUP_WORDS)
             nc.vector.quantize_mx(out=codes[:, group].bitcast(FP8X4), scales=scales[:, group], in_=stage[:])
 
-        def hidden_matmul(tt, g):
-            u_bank = work.tile([P, BANK], F32, tag="work")
-            for j in range(4):
-                for c in range(D_PASSES):
-                    w_cols = slice(g * GROUP_WORDS + (2 * j + c) * P, g * GROUP_WORDS + (2 * j + c + 1) * P)
-                    h_cols = slice((2 * tt + c) * P, (2 * tt + c + 1) * P)
-                    nc.tensor.matmul_mx(
-                        out=u_bank[:, j * P : (j + 1) * P],
-                        lhsT=wfc_codes[:, w_cols].bitcast(FP8X4),
-                        lhsT_scale=wfc_scales[:, w_cols],
-                        rhs=h_codes[:, h_cols].bitcast(FP8X4),
-                        rhs_scale=h_scales[:, h_cols],
-                        start=(c == 0),
-                        stop=(c == D_PASSES - 1),
-                    )
-            return u_bank
+        def hidden_matmul(out, tt, n, g, j):
+            for c in range(D_PASSES):
+                w_cols = slice(g * GROUP_WORDS + (2 * j + c) * P, g * GROUP_WORDS + (2 * j + c + 1) * P)
+                h_cols = slice(h_base(tt) + c * n * P, h_base(tt) + (c + 1) * n * P)
+                nc.tensor.matmul_mx(
+                    out=out,
+                    lhsT=wfc_codes[:, w_cols].bitcast(FP8X4),
+                    lhsT_scale=wfc_scales[:, w_cols],
+                    rhs=h_codes[:, h_cols].bitcast(FP8X4),
+                    rhs_scale=h_scales[:, h_cols],
+                    start=(c == 0),
+                    stop=(c == D_PASSES - 1),
+                )
 
-        def evacuate(u_bank, square, factor, ti, engine):
-            part = slice(ti * BANK, (ti + 1) * BANK)
-            words = u_bank[:].rearrange("p (j t) -> p t j", j=4)
-            nc.scalar.activation(out=square[:, part].rearrange("p (t j) -> p t j", j=4), in_=words, func=FUNC.Square)
-            factor_part = factor[:, part].rearrange("p (t j) -> p t j", j=4)
+        def take_square(square, words):
+            nc.scalar.activation(out=square, in_=words, func=FUNC.Square)
+
+        def take_factor(factor, words, engine):
             if engine == "scalar":
-                nc.scalar.activation(out=factor_part, in_=words, func=FUNC.Sign)
+                nc.scalar.activation(out=factor, in_=words, func=FUNC.Sign)
             else:
-                nc.vector.tensor_scalar(out=factor_part, in0=words, scalar1=0.0, scalar2=0.25, op0=ALU.is_ge, op1=ALU.max)
+                nc.vector.tensor_scalar(out=factor, in0=words, scalar1=0.0, scalar2=0.25, op0=ALU.is_ge, op1=ALU.max)
 
-        def multiply(n, square, factor, engine):
-            act_grouped = act_pool.tile([P, n * BANK], BF16, tag="act_grouped", align_bytes=64)
-            for ti in range(n):
-                if engine[ti] == "scalar":
-                    part = slice(ti * BANK, (ti + 1) * BANK)
-                    nc.vector.tensor_scalar(
-                        out=factor[:, part], in0=factor[:, part], scalar1=0.25, scalar2=None, op0=ALU.max
-                    )
-            nc.vector.tensor_tensor(out=act_grouped[:], in0=square[:], in1=factor[:], op=ALU.mult)
+        def hidden_half(tt, g, b, square, factor, engine, factor_first):
+            u_bank = new_bank()
+            for e in range(2):
+                hidden_matmul(u_bank[:, e * 2 * P : (e + 1) * 2 * P], tt, 2, g, 2 * b + e)
+            words = u_bank[:].rearrange("p (e t) -> p t e", e=2)
+            part = slice(b * BANK, (b + 1) * BANK)
+            square_part = square[:, part].rearrange("p (t e) -> p t e", e=2)
+            factor_part = factor[:, part].rearrange("p (t e) -> p t e", e=2)
+            if factor_first:
+                take_factor(factor_part, words, engine)
+            take_square(square_part, words)
+            if not factor_first:
+                take_factor(factor_part, words, engine)
+
+        def hidden_single(tt, g, engine):
+            square = act_pool.tile([P, 2 * BANK], BF16, tag="square")
+            factor = act_pool.tile([P, 2 * BANK], BF16, tag="factor")
+            u_bank = new_bank()
+            for j in range(4):
+                hidden_matmul(u_bank[:, j * P : (j + 1) * P], tt, 1, g, j)
+            words = u_bank[:].rearrange("p (j t) -> p t j", j=4)
+            take_square(square[:, 0:BANK].rearrange("p (t j) -> p t j", j=4), words)
+            take_factor(factor[:, 0:BANK].rearrange("p (t j) -> p t j", j=4), words, engine)
+            return square, factor
+
+        def clip_signs(n, factor, engines):
+            for b in range(n):
+                if engines[b] == "scalar" and not (b == 1 and engines[0] == "scalar"):
+                    last = n if engines == ("scalar", "scalar") else b + 1
+                    part = factor[:, b * BANK : last * BANK]
+                    nc.vector.tensor_scalar(out=part, in0=part, scalar1=0.25, scalar2=None, op0=ALU.max)
+
+        def multiply(n, square, factor):
+            act_grouped = act_pool.tile([P, 2 * BANK], BF16, tag="act_grouped", align_bytes=64)
+            if n == 2:
+                out_view = act_grouped[:].rearrange("p (t b e) -> p t b e", b=2, e=2)
+                square_view = square[:].rearrange("p (b t e) -> p t b e", b=2, e=2)
+                factor_view = factor[:].rearrange("p (b t e) -> p t b e", b=2, e=2)
+            else:
+                out_view, square_view, factor_view = act_grouped[:, 0:BANK], square[:, 0:BANK], factor[:, 0:BANK]
+            nc.vector.tensor_tensor(out=out_view, in0=square_view, in1=factor_view, op=ALU.mult)
             return act_grouped
 
         def quantise_act(n, act_grouped):
-            bufs = F_GROUPS if n == 2 else UNIT_CODES
-            act_codes = act_pool.tile([P, n * P], U32, tag="act_codes_%d" % n, align_bytes=64, bufs=bufs)
-            act_scales = act_pool.tile([P, n * P], U8, tag="act_scales_%d" % n, align_bytes=64, bufs=bufs)
-            nc.vector.quantize_mx(out=act_codes[:].bitcast(FP8X4), scales=act_scales[:], in_=act_grouped[:])
+            act_codes = act_pool.tile([P, 2 * P], U32, tag="act_codes", align_bytes=64, bufs=PAIR_CODES)
+            act_scales = act_pool.tile([P, 2 * P], U8, tag="act_scales", align_bytes=64, bufs=PAIR_CODES)
+            nc.vector.quantize_mx(
+                out=act_codes[:, 0 : n * P].bitcast(FP8X4), scales=act_scales[:, 0 : n * P], in_=act_grouped[:, 0 : n * BANK]
+            )
             return act_codes, act_scales
 
         sums = {}
 
         def project(tt, half, g, act):
-            act_codes, act_scales, ti, born = act
+            act_codes, act_scales = act
+            ti = tt % 2
             ring = (2 * tt + half) % ACC_BANKS
             if g == 0:
-                sums[(tt, half)] = acc_pool.tile([P, BANK], F32, name="sum_%d" % ring, tag="sum_%d" % ring)
+                if ring in work_banks:
+                    work_banks.remove(ring)
+                sums[(tt, half)] = psum.tile([P, BANK], F32, name="bank_%d" % ring, tag="bank_%d" % ring)
             w_cols = slice(g * GROUP_WORDS + half * BANK, g * GROUP_WORDS + (half + 1) * BANK)
             nc.tensor.matmul_mx(
                 out=sums[(tt, half)][:],
@@ -224,165 +277,177 @@ def tile_block_pc_kernel(tc, x_mid, wfc, wproj, mlp_scale, out):
                 stop=(g == F_GROUPS - 1),
             )
 
-        def finish(tt, half):
-            d_cols = slice(half * BANK, (half + 1) * BANK)
+        def apply_gain(tt, half):
             result = out_pool.tile([P, BANK], F32)
-            nc.vector.tensor_tensor(out=result[:], in0=sums[(tt, half)][:], in1=gain[:, d_cols], op=ALU.mult)
-            adder = nc.vector if ADDER == "vector" or tt == TOKEN_TILES - 1 else nc.gpsimd
-            adder.tensor_tensor(
+            nc.vector.tensor_tensor(
+                out=result[:], in0=sums[(tt, half)][:], in1=gain[:, half * BANK : (half + 1) * BANK], op=ALU.mult
+            )
+            return result
+
+        def add_residual(tt, half, result, engine):
+            cols = slice(half * BANK, (half + 1) * BANK)
+            engine.tensor_tensor(
                 out=result[:], in0=result[:], in1=x_sb[:, tt * D + half * BANK : tt * D + (half + 1) * BANK], op=ALU.add
             )
-            nc.sync.dma_start(out=out_rows[tt * P : (tt + 1) * P, d_cols], in_=result[:])
+            nc.sync.dma_start(out=out_rows[tt * P : (tt + 1) * P, cols], in_=result[:])
 
-        idle = keep.tile([P, BANK], BF16)
-        nc.gpsimd.memset(idle[:], 0.0)
+        zeros = keep.tile([P, BANK], BF16)
+        nc.gpsimd.memset(zeros[:], 0.0)
 
         def keep_warm(n):
-            bank = work.tile([P, BANK], F32, tag="work")
+            bank = new_bank()
             for i in range(n):
-                nc.tensor.matmul(bank[:], lhsT=idle[:, 0:P], rhs=idle[:], start=True, stop=True)
+                nc.tensor.matmul(bank[:], lhsT=zeros[:, 0:P], rhs=zeros[:], start=True, stop=True)
 
         make_identity(nc, ident_f32[:])
+        keep_warm(WARM[0])
         nc.vector.memset(eps12[:], 12.0e-6)
-        keep_warm(8)
         nc.scalar.activation(out=warm[:], in_=eps12[:], func=FUNC.Sqrt)
-        wfc_blocks = {}
-        wproj_blocks = {}
+        load_order = [("wfc", 0), ("wfc", 1)]
+        for g in range(F_GROUPS):
+            load_order += [("wfc", g + 2)] if g + 2 < F_GROUPS else []
+            load_order += [("wproj", g)]
+        blocks = {}
 
-        def load_pair(g):
-            wproj_blocks[g], wproj_blocks[g + 1] = load_wproj_pair(g)
+        def load_next():
+            if load_order:
+                kind, g = load_order.pop(0)
+                blocks[(kind, g)] = load_weights(kind, g)
+                if len(load_order) == X_AFTER:
+                    for tt in range(2, TOKEN_TILES):
+                        load_x(tt)
+                if not load_order:
+                    nc.sync.dma_start(out=gain[:], in_=mlp_scale.partition_broadcast(P))
 
         load_x(0)
         load_x(1)
-        wfc_blocks[0] = load_wfc(0)
-        wfc_blocks[1] = load_wfc(1)
-        wfc_blocks[2] = load_wfc(2)
-        load_pair(0)
-        wfc_blocks[3] = load_wfc(3)
+        for i in range(RAW_BUFS):
+            load_next()
+        stage = stage_pool.tile([P, 4 * GROUP_WORDS], BF16, tag="stage", align_bytes=64)
         square_sum(0, "scalar")
         square_sum(1, "vector")
         root(0)
         h_rows0 = scale_h(0)
         root(1)
         h_rows1 = scale_h(1)
+        banks = [transpose_bank(blocks[("wfc", 0)], b) for b in range(2)]
         bank0 = transpose_h(h_rows0)
-        h0 = group_h(bank0)
         bank1 = transpose_h(h_rows1)
+        copy_bank(stage, 0, banks[0], "scalar")
+        copy_bank(stage, 1, banks[1], "vector")
+        h0 = group_h(bank0)
         h1 = group_h(bank1)
-        stage = transpose_weights(wfc_blocks[0], ("scalar", "vector", "scalar", "vector"))
-        keep_warm(3)
+        banks += [transpose_bank(blocks[("wfc", 0)], b) for b in range(2, 4)]
+        load_next()
+        half = slice(0, GROUP_WORDS // 2)
+        nc.vector.quantize_mx(
+            out=wfc_codes[:, half].bitcast(FP8X4), scales=wfc_scales[:, half], in_=stage[:, 0 : 2 * GROUP_WORDS]
+        )
         quantise_h(0, h0)
         quantise_h(1, h1)
-        quantise_weights(stage, wfc_codes, wfc_scales, 0)
+        keep_warm(WARM[1])
+        copy_bank(stage, 2, banks[2], "scalar")
+        copy_bank(stage, 3, banks[3], "vector")
+        half = slice(GROUP_WORDS // 2, GROUP_WORDS)
+        nc.vector.quantize_mx(
+            out=wfc_codes[:, half].bitcast(FP8X4), scales=wfc_scales[:, half], in_=stage[:, 2 * GROUP_WORDS :]
+        )
 
-        acts = {}
-        pending = None
-        done = {}
+        steps = [(tt, n, g) for tt, n in ((0, 2), (2, 2), (4, 1)) for g in range(F_GROUPS)]
+        todo = [(tt, half, g) for g in range(F_GROUPS) for tt, half in EARLY]
+        for tt in range(4):
+            todo += [(tt, half, g) for g in range(F_GROUPS) for half in range(2) if (tt, half) not in EARLY]
+        todo += [(4, half, g) for half in range(2) for g in range(F_GROUPS)]
+        ready = {}
+        gained = []
 
-        def project_ready(tt, half, upto):
-            g = done.get((tt, half), 0)
-            while g <= upto and (tt, g) in acts:
-                project(tt, half, g, acts[(tt, g)])
-                g += 1
-            done[(tt, half)] = g
-
-        for g in range(F_GROUPS):
-            wf = g + 1
-            wp = g - 1
-            if wf < F_GROUPS:
-                if wf + 3 < F_GROUPS:
-                    wfc_blocks[wf + 3] = load_wfc(wf + 3)
-                if wf == 1:
-                    load_pair(2)
-                stage = transpose_weights(wfc_blocks[wf], WFC_ENGINES)
-            if pending is not None:
-                act_grouped = multiply(2, pending[1], pending[2], PAIR_ENGINES)
-            if wf < F_GROUPS:
-                quantise_weights(stage, wfc_codes, wfc_scales, wf)
-            for tt, half in EARLY:
-                project_ready(tt, half, g - 3)
-            if g < 3:
-                keep_warm(3)
-            if pending is not None:
-                codes, scales = quantise_act(2, act_grouped)
-                acts[(0, pending[0])] = (codes, scales, 0, 0)
-                acts[(1, pending[0])] = (codes, scales, 1, 0)
-            if wp >= 0:
-                stage = transpose_weights(wproj_blocks[wp], WPROJ_ENGINES)
-                if wp in (1, 3):
-                    load_pair(wp + 3)
-            square = act_pool.tile([P, 2 * BANK], BF16, tag="square")
-            factor = act_pool.tile([P, 2 * BANK], BF16, tag="factor")
-            banks = [hidden_matmul(tt, g) for tt in range(2)]
-            for ti in range(2):
-                evacuate(banks[ti], square, factor, ti, PAIR_ENGINES[ti])
-            if wp >= 0:
-                quantise_weights(stage, wproj_codes, wproj_scales, wp)
-            pending = (g, square, factor)
-            if g == 3:
-                for tt in range(2, TOKEN_TILES):
-                    load_x(tt)
-            if g == 4:
-                nc.sync.dma_start(out=gain[:], in_=mlp_scale.partition_broadcast(P))
-            if g == 4:
-                square_sum(2, "scalar")
-                root(2)
-            if g == 5:
-                h_rows = scale_h(2)
-            if g == 6:
-                h1 = group_h(transpose_h(h_rows))
-            if g == 7:
-                quantise_h(2, h1)
-
-        units = [(tt, g) for tt in range(2, TOKEN_TILES) for g in range(F_GROUPS)]
-        todo = []
-        for tt, half in EARLY:
-            todo += [(tt, half, g) for g in range(done[(tt, half)], F_GROUPS)]
-        todo.sort(key=lambda k: (k[2], k[0], k[1]))
-        for half in range(2):
-            if (1, half) not in EARLY:
-                todo += [(1, half, g) for g in range(F_GROUPS)]
-        todo += [(tt, half, g) for tt in range(2, TOKEN_TILES) for g in range(F_GROUPS) for half in range(2)]
-
-        def some_projects(n, age):
-            while n > 0 and todo and (todo[0][0], todo[0][2]) in acts and acts[(todo[0][0], todo[0][2])][3] <= age:
-                tt, half, g = todo.pop(0)
-                project(tt, half, g, acts[(tt, g)])
+        def projects(n, step):
+            while n > 0 and todo:
+                tt, half, g = todo[0]
+                if (tt, g) not in ready or ready[(tt, g)][0] > step:
+                    return
+                todo.pop(0)
+                project(tt, half, g, ready[(tt, g)][1])
                 n -= 1
                 if g == F_GROUPS - 1:
-                    finish(tt, half)
+                    gained.append((tt, half, apply_gain(tt, half)))
 
-        pending = (0, 2, F_GROUPS - 1, square, factor, PAIR_ENGINES)
-        h_at = {}
-        for n, (tt, g) in enumerate(units):
-            if n == 0:
-                stage = transpose_weights(wproj_blocks[F_GROUPS - 1], WPROJ_ENGINES)
-            u_bank = hidden_matmul(tt, g)
-            engine = UNIT_ENGINES[n % len(UNIT_ENGINES)]
-            square = act_pool.tile([P, BANK], BF16, tag="square")
-            factor = act_pool.tile([P, BANK], BF16, tag="factor")
-            evacuate(u_bank, square, factor, 0, engine)
-            t0, nt, g0, sq0, fa0, en0 = pending
-            act_grouped = multiply(nt, sq0, fa0, en0)
-            if n == 0:
-                quantise_weights(stage, wproj_codes, wproj_scales, F_GROUPS - 1)
-            if tt + 1 < TOKEN_TILES:
-                if g == H_STEPS[0]:
-                    square_sum(tt + 1, "scalar")
-                if g == H_STEPS[1]:
-                    root(tt + 1)
-                if g == H_STEPS[2]:
-                    h_rows = scale_h(tt + 1)
-                if g == H_STEPS[3]:
-                    h1 = group_h(transpose_h(h_rows))
-                if g == H_STEPS[4]:
-                    quantise_h(tt + 1, h1)
-            codes, scales = quantise_act(nt, act_grouped)
-            for ti in range(nt):
-                acts[(t0 + ti, g0)] = (codes, scales, ti, n)
-            some_projects(-(-(len(todo) - 2 * UNIT_LAG) // (len(units) - n)), n - UNIT_LAG)
-            pending = (tt, 1, g, square, factor, (engine,))
-        t0, nt, g0, sq0, fa0, en0 = pending
-        codes, scales = quantise_act(nt, multiply(nt, sq0, fa0, en0))
-        acts[(t0, g0)] = (codes, scales, 0, 0)
-        some_projects(1000, 1000)
+        h_parts = {}
+        queue = []
+        stage_wp = None
+
+        def h_work(s, i):
+            for t, at in H_AT:
+                if at[i] == s:
+                    if i == 0:
+                        square_sum(t, "scalar")
+                    if i == 1:
+                        root(t)
+                    if i == 2:
+                        h_parts[t] = scale_h(t)
+                    if i == 3:
+                        h_parts[t] = group_h(transpose_h(h_parts[t]))
+                    if i == 4:
+                        quantise_h(t, h_parts[t])
+
+        def quantise_oldest(s):
+            tt, n, g, grouped = queue[0][0], queue[0][1], queue[0][2], queue[0][6]
+            queue.pop(0)
+            act = quantise_act(n, grouped)
+            for ti in range(n):
+                ready[(tt + ti, g)] = (s, act)
+
+        for s in range(len(steps)):
+            tt, n, g = steps[s]
+            wf = s + 1
+            wp = s - 1
+            early_step = s < F_GROUPS
+            engines = FACTOR_1 if early_step else (FACTOR_2 if n == 2 else (FACTOR_3,))
+            if n == 2:
+                square = act_pool.tile([P, 2 * BANK], BF16, tag="square")
+                factor = act_pool.tile([P, 2 * BANK], BF16, tag="factor")
+            if wf < F_GROUPS:
+                stage = transpose_weights(blocks[("wfc", wf)], WFC_ENGINES)
+                load_next()
+            h_work(s, 2)
+            if n == 2:
+                hidden_half(tt, g, 0, square, factor, engines[0], FIRST_0)
+            if early_step and s >= FIRST_PROJECT:
+                projects(EARLY_PROJECTS[0], s - 1)
+            if len(queue) > 1:
+                quantise_oldest(s)
+            if queue:
+                queue[-1][6] = multiply(queue[-1][1], queue[-1][3], queue[-1][4])
+            h_work(s, 4)
+            if wf < F_GROUPS:
+                quantise_weights(stage, wfc_codes, wfc_scales, wf)
+            while gained:
+                add_residual(*gained.pop(0), nc.vector)
+            h_work(s, 0)
+            h_work(s, 1)
+            if 0 <= wp < F_GROUPS:
+                stage_wp = transpose_weights(blocks[("wproj", wp)], WPROJ_ENGINES)
+                load_next()
+            h_work(s, 3)
+            if n == 2:
+                hidden_half(tt, g, 1, square, factor, engines[1], FIRST_1)
+            else:
+                square, factor = hidden_single(tt, g, FACTOR_3)
+            if early_step and s >= FIRST_PROJECT:
+                projects(EARLY_PROJECTS[1], s - 1)
+            if 0 <= wp < F_GROUPS:
+                quantise_weights(stage_wp, wproj_codes, wproj_scales, wp)
+            if not early_step:
+                left = len(steps) - s
+                weight = 2 * (2 * F_GROUPS - s) + F_GROUPS if s < 2 * F_GROUPS else left
+                quota = -(-(len(todo) - TAIL) * (2 if n == 2 else 1) // weight)
+                projects(quota, s - 1)
+            clip_signs(n, factor, engines)
+            queue.append([tt, n, g, square, factor, engines, None])
+        quantise_oldest(0)
+        queue[-1][6] = multiply(1, queue[-1][3], queue[-1][4])
+        projects(3, 1000)
+        quantise_oldest(0)
+        projects(1000, 1000)
+        while gained:
+            add_residual(*gained.pop(0), nc.vector)

@@ -21,22 +21,24 @@ D_PASSES = D // K_PASS
 F_GROUPS = F // K_PASS
 TOKEN_TILES = T // P
 GROUP_WORDS = 1024
-ACC_BANKS = 3
+RING = (0, 1, 2, 0, 1, 2, 3, 0, 1, 2)
 PAIR_CODES = 12
 RAW_BUFS = 7
 WARM = (8, 2)
 FIRST_0 = False
+FIRST_1_LATE = False
 FIRST_1 = True
 X_AFTER = 10
 FIRST_PROJECT = 3
 EARLY_PROJECTS = (2, 1)
 EARLY = ((0, 0), (0, 1), (1, 0))
-WFC_ENGINES = ("scalar", "scalar", "vector", "scalar")
+WFC_ENGINES = ("scalar", "vector", "scalar", "scalar")
 WPROJ_ENGINES = ("scalar", "scalar", "vector", "scalar")
 FACTOR_1 = ("vector", "scalar")
-FACTOR_2 = ("scalar", "scalar")
-FACTOR_3 = "scalar"
-TAIL = 6
+FACTOR_2 = (("scalar", "vector"), ("scalar", "scalar"))
+FACTOR_3 = ("scalar", "scalar")
+TAIL = 20
+Q_PARTS = 2
 H_AT = ((2, (4, 4, 5, 6, 7)), (3, (5, 5, 6, 6, 7)), (4, (9, 9, 10, 12, 13)))
 
 FLOPS = 2 * 2 * T * D * F
@@ -48,10 +50,10 @@ def tile_block_pc_kernel(tc, x_mid, wfc, wproj, mlp_scale, out):
     out_rows = out.flatten_outer_dims()
 
     with ExitStack() as pools:
-        pools.enter_context(tc.manual_schedule(engines={mybir.EngineType.PE}))
+        pools.enter_context(tc.manual_schedule(engines={mybir.EngineType.PE, mybir.EngineType.Activation}))
         keep = pools.enter_context(tc.tile_pool(name="keep", bufs=1))
         raw_pool = pools.enter_context(tc.tile_pool(name="raw", bufs=RAW_BUFS))
-        stage_pool = pools.enter_context(tc.tile_pool(name="stage", bufs=3))
+        stage_pool = pools.enter_context(tc.tile_pool(name="stage", bufs=2))
         norm_pool = pools.enter_context(tc.tile_pool(name="norm", bufs=2))
         act_pool = pools.enter_context(tc.tile_pool(name="act", bufs=3))
         out_pool = pools.enter_context(tc.tile_pool(name="outp", bufs=3))
@@ -179,8 +181,14 @@ def tile_block_pc_kernel(tc, x_mid, wfc, wproj, mlp_scale, out):
             return stage
 
         def quantise_weights(stage, codes, scales, g):
-            group = slice(g * GROUP_WORDS, (g + 1) * GROUP_WORDS)
-            nc.vector.quantize_mx(out=codes[:, group].bitcast(FP8X4), scales=scales[:, group], in_=stage[:])
+            for part in range(Q_PARTS):
+                width = GROUP_WORDS // Q_PARTS
+                cols = slice(g * GROUP_WORDS + part * width, g * GROUP_WORDS + (part + 1) * width)
+                nc.vector.quantize_mx(
+                    out=codes[:, cols].bitcast(FP8X4),
+                    scales=scales[:, cols],
+                    in_=stage[:, part * 4 * width : (part + 1) * 4 * width],
+                )
 
         def hidden_matmul(out, tt, n, g, j):
             for c in range(D_PASSES):
@@ -261,7 +269,7 @@ def tile_block_pc_kernel(tc, x_mid, wfc, wproj, mlp_scale, out):
         def project(tt, half, g, act):
             act_codes, act_scales = act
             ti = tt % 2
-            ring = (2 * tt + half) % ACC_BANKS
+            ring = RING[2 * tt + half]
             if g == 0:
                 if ring in work_banks:
                     work_banks.remove(ring)
@@ -402,7 +410,7 @@ def tile_block_pc_kernel(tc, x_mid, wfc, wproj, mlp_scale, out):
             wf = s + 1
             wp = s - 1
             early_step = s < F_GROUPS
-            engines = FACTOR_1 if early_step else (FACTOR_2 if n == 2 else (FACTOR_3,))
+            engines = FACTOR_1 if early_step else (FACTOR_2[g % 2] if n == 2 else (FACTOR_3[g % 2],))
             if n == 2:
                 square = act_pool.tile([P, 2 * BANK], BF16, tag="square")
                 factor = act_pool.tile([P, 2 * BANK], BF16, tag="factor")
@@ -430,9 +438,9 @@ def tile_block_pc_kernel(tc, x_mid, wfc, wproj, mlp_scale, out):
                 load_next()
             h_work(s, 3)
             if n == 2:
-                hidden_half(tt, g, 1, square, factor, engines[1], FIRST_1)
+                hidden_half(tt, g, 1, square, factor, engines[1], FIRST_1 if early_step else FIRST_1_LATE)
             else:
-                square, factor = hidden_single(tt, g, FACTOR_3)
+                square, factor = hidden_single(tt, g, engines[0])
             if early_step and s >= FIRST_PROJECT:
                 projects(EARLY_PROJECTS[1], s - 1)
             if 0 <= wp < F_GROUPS:

@@ -23,23 +23,24 @@ TOKEN_TILES = T // P
 GROUP_WORDS = 1024
 RING = (0, 1, 2, 0, 1, 2, 3, 0, 1, 2)
 PAIR_CODES = 12
-RAW_BUFS = 7
-WARM = (8, 2)
+RAW_BUFS = 6
+WARM = (8, 0, 2)
+STEP_WARM = ()
 FIRST_0 = False
 FIRST_1_LATE = False
 FIRST_1 = True
-X_AFTER = 10
+X_AFTER = 7
 FIRST_PROJECT = 3
 EARLY_PROJECTS = (2, 1)
 EARLY = ((0, 0), (0, 1), (1, 0))
 WFC_ENGINES = ("scalar", "vector", "scalar", "scalar")
-WPROJ_ENGINES = ("scalar", "scalar", "vector", "scalar")
+WPROJ_ENGINES = ("scalar", "scalar", "scalar", "vector")
 FACTOR_1 = ("vector", "scalar")
 FACTOR_2 = (("scalar", "vector"), ("scalar", "scalar"))
 FACTOR_3 = ("scalar", "scalar")
-TAIL = 20
+TAIL = (20, 20)
 Q_PARTS = 2
-H_AT = ((2, (4, 4, 5, 6, 7)), (3, (5, 5, 6, 6, 7)), (4, (9, 9, 10, 12, 13)))
+H_AT = ((2, 2, (4, 4, 5, 6, 7)), (4, 1, (9, 9, 10, 12, 13)))
 
 FLOPS = 2 * 2 * T * D * F
 
@@ -116,13 +117,15 @@ def tile_block_pc_kernel(tc, x_mid, wfc, wproj, mlp_scale, out):
                     accum_out=sumsq[:, tt : tt + 1],
                 )
 
-        def root(tt):
+        def root(tt, n):
             nc.scalar.activation(
-                out=rms[:, tt : tt + 1], in_=sumsq[:, tt : tt + 1], func=FUNC.Sqrt, scale=12.0 / D, bias=eps12[:]
+                out=rms[:, tt : tt + n], in_=sumsq[:, tt : tt + n], func=FUNC.Sqrt, scale=12.0 / D, bias=eps12[:]
             )
 
+        def reciprocal(tt, n):
+            nc.vector.reciprocal(out=rstd[:, tt : tt + n], in_=rms[:, tt : tt + n])
+
         def scale_h(tt):
-            nc.vector.reciprocal(out=rstd[:, tt : tt + 1], in_=rms[:, tt : tt + 1])
             h_rows = norm_pool.tile([P, D], BF16)
             nc.vector.tensor_scalar(
                 out=h_rows[:], in0=x_sb[:, tt * D : (tt + 1) * D], scalar1=rstd[:, tt : tt + 1], scalar2=None, op0=ALU.mult
@@ -136,28 +139,17 @@ def tile_block_pc_kernel(tc, x_mid, wfc, wproj, mlp_scale, out):
                 nc.tensor.transpose(h_bank[:, n * P : (n + 1) * P], words[:, n * P : (n + 1) * P], ident_f32[:])
             return h_bank
 
-        def group_h(h_bank):
-            h_grouped = norm_pool.tile([P, D], BF16, align_bytes=64)
+        def group_h(h_bank, h_grouped, n, ti):
             nc.scalar.copy(
-                out=h_grouped[:].bitcast(F32).rearrange("p (c t u) -> p c t u", c=2, u=2),
+                out=h_grouped[:, 0 : n * D].bitcast(F32).rearrange("p (c i t u) -> p c i t u", c=2, i=n, u=2)[:, :, ti, :, :],
                 in_=h_bank[:].rearrange("p (c u t) -> p c t u", c=2, u=2),
             )
-            return h_grouped
 
-        def h_base(tt):
-            return (tt // 2) * 2 * D_PASSES * P + (tt % 2) * P
-
-        def h_step(tt):
-            return 2 * P if tt < 4 else P
-
-        def quantise_h(tt, h_grouped):
-            for c in range(D_PASSES):
-                cols = slice(h_base(tt) + c * h_step(tt), h_base(tt) + c * h_step(tt) + P)
-                nc.vector.quantize_mx(
-                    out=h_codes[:, cols].bitcast(FP8X4),
-                    scales=h_scales[:, cols],
-                    in_=h_grouped[:, c * K_PASS : (c + 1) * K_PASS],
-                )
+        def quantise_h(tt, n, h_grouped):
+            cols = slice(tt * 2 * P, (tt + n) * 2 * P)
+            nc.vector.quantize_mx(
+                out=h_codes[:, cols].bitcast(FP8X4), scales=h_scales[:, cols], in_=h_grouped[:, 0 : n * D]
+            )
 
         def transpose_bank(blocks, b):
             bank = new_bank()
@@ -193,7 +185,7 @@ def tile_block_pc_kernel(tc, x_mid, wfc, wproj, mlp_scale, out):
         def hidden_matmul(out, tt, n, g, j):
             for c in range(D_PASSES):
                 w_cols = slice(g * GROUP_WORDS + (2 * j + c) * P, g * GROUP_WORDS + (2 * j + c + 1) * P)
-                h_cols = slice(h_base(tt) + c * n * P, h_base(tt) + (c + 1) * n * P)
+                h_cols = slice((2 * tt + c * n) * P, (2 * tt + (c + 1) * n) * P)
                 nc.tensor.matmul_mx(
                     out=out,
                     lhsT=wfc_codes[:, w_cols].bitcast(FP8X4),
@@ -285,24 +277,36 @@ def tile_block_pc_kernel(tc, x_mid, wfc, wproj, mlp_scale, out):
                 stop=(g == F_GROUPS - 1),
             )
 
-        def apply_gain(tt, half):
-            result = out_pool.tile([P, BANK], F32)
-            nc.vector.tensor_tensor(
-                out=result[:], in0=sums[(tt, half)][:], in1=gain[:, half * BANK : (half + 1) * BANK], op=ALU.mult
-            )
-            return result
+        results = {}
 
-        def add_residual(tt, half, result, engine):
-            cols = slice(half * BANK, (half + 1) * BANK)
-            engine.tensor_tensor(
-                out=result[:], in0=result[:], in1=x_sb[:, tt * D + half * BANK : tt * D + (half + 1) * BANK], op=ALU.add
+        def apply_gain(tt, half):
+            if half == 0:
+                results[tt] = out_pool.tile([P, D], F32, name="result", tag="result")
+            pieces = 2 if (tt, half) == (TOKEN_TILES - 1, 1) else 1
+            width = BANK // pieces
+            for i in range(pieces):
+                cols = slice(half * BANK + i * width, half * BANK + (i + 1) * width)
+                nc.vector.tensor_tensor(
+                    out=results[tt][:, cols],
+                    in0=sums[(tt, half)][:, i * width : (i + 1) * width],
+                    in1=gain[:, cols],
+                    op=ALU.mult,
+                )
+
+        def add_residual(tt, first, width):
+            cols = slice(first, first + width)
+            part = results[tt][:, cols]
+            nc.vector.tensor_tensor(
+                out=part, in0=part, in1=x_sb[:, tt * D + first : tt * D + first + width], op=ALU.add
             )
-            nc.sync.dma_start(out=out_rows[tt * P : (tt + 1) * P, cols], in_=result[:])
+            nc.sync.dma_start(out=out_rows[tt * P : (tt + 1) * P, cols], in_=part)
 
         zeros = keep.tile([P, BANK], BF16)
         nc.gpsimd.memset(zeros[:], 0.0)
 
         def keep_warm(n):
+            if n == 0:
+                return
             bank = new_bank()
             for i in range(n):
                 nc.tensor.matmul(bank[:], lhsT=zeros[:, 0:P], rhs=zeros[:], start=True, stop=True)
@@ -334,25 +338,28 @@ def tile_block_pc_kernel(tc, x_mid, wfc, wproj, mlp_scale, out):
         stage = stage_pool.tile([P, 4 * GROUP_WORDS], BF16, tag="stage", align_bytes=64)
         square_sum(0, "scalar")
         square_sum(1, "vector")
-        root(0)
+        root(0, 1)
+        reciprocal(0, 1)
         h_rows0 = scale_h(0)
-        root(1)
+        root(1, 1)
+        reciprocal(1, 1)
         h_rows1 = scale_h(1)
         banks = [transpose_bank(blocks[("wfc", 0)], b) for b in range(2)]
         bank0 = transpose_h(h_rows0)
+        keep_warm(WARM[2])
         bank1 = transpose_h(h_rows1)
         copy_bank(stage, 0, banks[0], "scalar")
         copy_bank(stage, 1, banks[1], "vector")
-        h0 = group_h(bank0)
-        h1 = group_h(bank1)
+        h_first = norm_pool.tile([P, 2 * D], BF16, tag="h_grouped", align_bytes=64)
+        group_h(bank0, h_first, 2, 0)
+        group_h(bank1, h_first, 2, 1)
         banks += [transpose_bank(blocks[("wfc", 0)], b) for b in range(2, 4)]
         load_next()
         half = slice(0, GROUP_WORDS // 2)
         nc.vector.quantize_mx(
             out=wfc_codes[:, half].bitcast(FP8X4), scales=wfc_scales[:, half], in_=stage[:, 0 : 2 * GROUP_WORDS]
         )
-        quantise_h(0, h0)
-        quantise_h(1, h1)
+        quantise_h(0, 2, h_first)
         keep_warm(WARM[1])
         copy_bank(stage, 2, banks[2], "scalar")
         copy_bank(stage, 3, banks[3], "vector")
@@ -378,25 +385,37 @@ def tile_block_pc_kernel(tc, x_mid, wfc, wproj, mlp_scale, out):
                 project(tt, half, g, ready[(tt, g)][1])
                 n -= 1
                 if g == F_GROUPS - 1:
-                    gained.append((tt, half, apply_gain(tt, half)))
+                    apply_gain(tt, half)
+                    if (tt, half) == (TOKEN_TILES - 1, 0):
+                        gained.append((tt, 0, BANK))
+                    elif tt == TOKEN_TILES - 1:
+                        gained.extend([(tt, BANK, BANK // 2), (tt, BANK + BANK // 2, BANK // 2)])
+                    elif half == 1:
+                        gained.append((tt, 0, D))
 
         h_parts = {}
         queue = []
         stage_wp = None
 
         def h_work(s, i):
-            for t, at in H_AT:
-                if at[i] == s:
-                    if i == 0:
-                        square_sum(t, "scalar")
-                    if i == 1:
-                        root(t)
-                    if i == 2:
-                        h_parts[t] = scale_h(t)
-                    if i == 3:
-                        h_parts[t] = group_h(transpose_h(h_parts[t]))
-                    if i == 4:
-                        quantise_h(t, h_parts[t])
+            for t, n, at in H_AT:
+                if at[i] != s:
+                    continue
+                if i == 0:
+                    for ti in range(n):
+                        square_sum(t + ti, "scalar")
+                if i == 1:
+                    root(t, n)
+                if i == 2:
+                    reciprocal(t, n)
+                    h_parts[t] = [scale_h(t + ti) for ti in range(n)]
+                if i == 3:
+                    h_grouped = norm_pool.tile([P, 2 * D], BF16, tag="h_grouped", align_bytes=64)
+                    for ti in range(n):
+                        group_h(transpose_h(h_parts[t][ti]), h_grouped, n, ti)
+                    h_parts[t] = h_grouped
+                if i == 4:
+                    quantise_h(t, n, h_parts[t])
 
         def quantise_oldest(s):
             tt, n, g, grouped = queue[0][0], queue[0][1], queue[0][2], queue[0][6]
@@ -418,6 +437,8 @@ def tile_block_pc_kernel(tc, x_mid, wfc, wproj, mlp_scale, out):
                 stage = transpose_weights(blocks[("wfc", wf)], WFC_ENGINES)
                 load_next()
             h_work(s, 2)
+            if s < len(STEP_WARM):
+                keep_warm(STEP_WARM[s])
             if n == 2:
                 hidden_half(tt, g, 0, square, factor, engines[0], FIRST_0)
             if early_step and s >= FIRST_PROJECT:
@@ -430,7 +451,7 @@ def tile_block_pc_kernel(tc, x_mid, wfc, wproj, mlp_scale, out):
             if wf < F_GROUPS:
                 quantise_weights(stage, wfc_codes, wfc_scales, wf)
             while gained:
-                add_residual(*gained.pop(0), nc.vector)
+                add_residual(*gained.pop(0))
             h_work(s, 0)
             h_work(s, 1)
             if 0 <= wp < F_GROUPS:
@@ -448,7 +469,7 @@ def tile_block_pc_kernel(tc, x_mid, wfc, wproj, mlp_scale, out):
             if not early_step:
                 left = len(steps) - s
                 weight = 2 * (2 * F_GROUPS - s) + F_GROUPS if s < 2 * F_GROUPS else left
-                quota = -(-(len(todo) - TAIL) * (2 if n == 2 else 1) // weight)
+                quota = -(-(len(todo) - TAIL[2 - n]) * (2 if n == 2 else 1) // weight)
                 projects(quota, s - 1)
             clip_signs(n, factor, engines)
             queue.append([tt, n, g, square, factor, engines, None])
@@ -458,4 +479,4 @@ def tile_block_pc_kernel(tc, x_mid, wfc, wproj, mlp_scale, out):
         quantise_oldest(0)
         projects(1000, 1000)
         while gained:
-            add_residual(*gained.pop(0), nc.vector)
+            add_residual(*gained.pop(0))

@@ -22,9 +22,9 @@ F_GROUPS = F // K_PASS
 TOKEN_TILES = T // P
 GROUP_WORDS = 1024
 RING = (0, 1, 2, 0, 1, 2, 3, 0, 1, 2)
-PAIR_CODES = 12
-RAW_BUFS = 6
-WARM = (8, 0, 2)
+PAIR_CODES = 14
+RAW_BUFS = 5
+WARM = (5, 0, 2)
 STEP_WARM = ()
 FIRST_0 = False
 FIRST_1_LATE = False
@@ -38,7 +38,8 @@ WPROJ_ENGINES = ("scalar", "scalar", "scalar", "vector")
 FACTOR_1 = ("vector", "scalar")
 FACTOR_2 = (("scalar", "vector"), ("scalar", "scalar"))
 FACTOR_3 = ("scalar", "scalar")
-TAIL = (20, 20)
+QUOTA = (4, 1)
+SKIP = ()
 Q_PARTS = 2
 H_AT = ((2, 2, (4, 4, 5, 6, 7)), (4, 1, (9, 9, 10, 12, 13)))
 
@@ -56,7 +57,7 @@ def tile_block_pc_kernel(tc, x_mid, wfc, wproj, mlp_scale, out):
         raw_pool = pools.enter_context(tc.tile_pool(name="raw", bufs=RAW_BUFS))
         stage_pool = pools.enter_context(tc.tile_pool(name="stage", bufs=2))
         norm_pool = pools.enter_context(tc.tile_pool(name="norm", bufs=2))
-        act_pool = pools.enter_context(tc.tile_pool(name="act", bufs=3))
+        act_pool = pools.enter_context(tc.tile_pool(name="act", bufs=4))
         out_pool = pools.enter_context(tc.tile_pool(name="outp", bufs=3))
         psum = pools.enter_context(tc.psum_pool(name="psum", bufs=1))
         work_banks = list(range(8))
@@ -70,12 +71,12 @@ def tile_block_pc_kernel(tc, x_mid, wfc, wproj, mlp_scale, out):
 
         x_sb = keep.tile([P, TOKEN_TILES * D], BF16)
         gain = keep.tile([P, D], BF16)
-        h_codes = keep.tile([P, TOKEN_TILES * D_PASSES * P], U32, align_bytes=64)
-        h_scales = keep.tile([P, TOKEN_TILES * D_PASSES * P], U8, align_bytes=64)
-        wfc_codes = keep.tile([P, F_GROUPS * GROUP_WORDS], U32, align_bytes=64)
-        wfc_scales = keep.tile([P, F_GROUPS * GROUP_WORDS], U8, align_bytes=64)
-        wproj_codes = keep.tile([P, F_GROUPS * GROUP_WORDS], U32, align_bytes=64)
-        wproj_scales = keep.tile([P, F_GROUPS * GROUP_WORDS], U8, align_bytes=64)
+        h_codes = keep.tile([P, TOKEN_TILES * D_PASSES * P], U32, align_bytes=256)
+        h_scales = keep.tile([P, TOKEN_TILES * D_PASSES * P], U8, align_bytes=256)
+        wfc_codes = keep.tile([P, F_GROUPS * GROUP_WORDS], U32, align_bytes=256)
+        wfc_scales = keep.tile([P, F_GROUPS * GROUP_WORDS], U8, align_bytes=256)
+        wproj_codes = keep.tile([P, F_GROUPS * GROUP_WORDS], U32, align_bytes=256)
+        wproj_scales = keep.tile([P, F_GROUPS * GROUP_WORDS], U8, align_bytes=256)
         sumsq = keep.tile([P, TOKEN_TILES], F32)
         rms = keep.tile([P, TOKEN_TILES], F32)
         rstd = keep.tile([P, TOKEN_TILES], F32)
@@ -166,7 +167,7 @@ def tile_block_pc_kernel(tc, x_mid, wfc, wproj, mlp_scale, out):
                 nc.vector.tensor_copy(out=stage_part, in_=bank_view)
 
         def transpose_weights(blocks, engines):
-            stage = stage_pool.tile([P, 4 * GROUP_WORDS], BF16, tag="stage", align_bytes=64)
+            stage = stage_pool.tile([P, 4 * GROUP_WORDS], BF16, tag="stage", align_bytes=256)
             banks = [transpose_bank(blocks, b) for b in range(4)]
             for b in range(4):
                 copy_bank(stage, b, banks[b], engines[b])
@@ -238,7 +239,7 @@ def tile_block_pc_kernel(tc, x_mid, wfc, wproj, mlp_scale, out):
                     nc.vector.tensor_scalar(out=part, in0=part, scalar1=0.25, scalar2=None, op0=ALU.max)
 
         def multiply(n, square, factor):
-            act_grouped = act_pool.tile([P, 2 * BANK], BF16, tag="act_grouped", align_bytes=64)
+            act_grouped = act_pool.tile([P, 2 * BANK], BF16, tag="act_grouped", align_bytes=256)
             if n == 2:
                 out_view = act_grouped[:].rearrange("p (t b e) -> p t b e", b=2, e=2)
                 square_view = square[:].rearrange("p (b t e) -> p t b e", b=2, e=2)
@@ -249,8 +250,8 @@ def tile_block_pc_kernel(tc, x_mid, wfc, wproj, mlp_scale, out):
             return act_grouped
 
         def quantise_act(n, act_grouped):
-            act_codes = act_pool.tile([P, 2 * P], U32, tag="act_codes", align_bytes=64, bufs=PAIR_CODES)
-            act_scales = act_pool.tile([P, 2 * P], U8, tag="act_scales", align_bytes=64, bufs=PAIR_CODES)
+            act_codes = act_pool.tile([P, 2 * P], U32, tag="act_codes", align_bytes=256, bufs=PAIR_CODES)
+            act_scales = act_pool.tile([P, 2 * P], U8, tag="act_scales", align_bytes=256, bufs=PAIR_CODES)
             nc.vector.quantize_mx(
                 out=act_codes[:, 0 : n * P].bitcast(FP8X4), scales=act_scales[:, 0 : n * P], in_=act_grouped[:, 0 : n * BANK]
             )
@@ -335,7 +336,7 @@ def tile_block_pc_kernel(tc, x_mid, wfc, wproj, mlp_scale, out):
         load_x(1)
         for i in range(RAW_BUFS):
             load_next()
-        stage = stage_pool.tile([P, 4 * GROUP_WORDS], BF16, tag="stage", align_bytes=64)
+        stage = stage_pool.tile([P, 4 * GROUP_WORDS], BF16, tag="stage", align_bytes=256)
         square_sum(0, "scalar")
         square_sum(1, "vector")
         root(0, 1)
@@ -350,7 +351,7 @@ def tile_block_pc_kernel(tc, x_mid, wfc, wproj, mlp_scale, out):
         bank1 = transpose_h(h_rows1)
         copy_bank(stage, 0, banks[0], "scalar")
         copy_bank(stage, 1, banks[1], "vector")
-        h_first = norm_pool.tile([P, 2 * D], BF16, tag="h_grouped", align_bytes=64)
+        h_first = norm_pool.tile([P, 2 * D], BF16, tag="h_grouped", align_bytes=256)
         group_h(bank0, h_first, 2, 0)
         group_h(bank1, h_first, 2, 1)
         banks += [transpose_bank(blocks[("wfc", 0)], b) for b in range(2, 4)]
@@ -410,7 +411,7 @@ def tile_block_pc_kernel(tc, x_mid, wfc, wproj, mlp_scale, out):
                     reciprocal(t, n)
                     h_parts[t] = [scale_h(t + ti) for ti in range(n)]
                 if i == 3:
-                    h_grouped = norm_pool.tile([P, 2 * D], BF16, tag="h_grouped", align_bytes=64)
+                    h_grouped = norm_pool.tile([P, 2 * D], BF16, tag="h_grouped", align_bytes=256)
                     for ti in range(n):
                         group_h(transpose_h(h_parts[t][ti]), h_grouped, n, ti)
                     h_parts[t] = h_grouped
@@ -424,12 +425,16 @@ def tile_block_pc_kernel(tc, x_mid, wfc, wproj, mlp_scale, out):
             for ti in range(n):
                 ready[(tt + ti, g)] = (s, act)
 
-        for s in range(len(steps)):
-            tt, n, g = steps[s]
+        plan = []
+        left = list(steps)
+        while left or len(plan) <= F_GROUPS:
+            plan.append(None if len(plan) in SKIP or not left else left.pop(0))
+        for s in range(len(plan)):
             wf = s + 1
             wp = s - 1
             early_step = s < F_GROUPS
-            engines = FACTOR_1 if early_step else (FACTOR_2[g % 2] if n == 2 else (FACTOR_3[g % 2],))
+            tt, n, g = plan[s] or (0, 0, 0)
+            engines = FACTOR_1 if early_step else (FACTOR_2[s % 2] if n == 2 else (FACTOR_3[s % 2],))
             if n == 2:
                 square = act_pool.tile([P, 2 * BANK], BF16, tag="square")
                 factor = act_pool.tile([P, 2 * BANK], BF16, tag="factor")
@@ -443,9 +448,9 @@ def tile_block_pc_kernel(tc, x_mid, wfc, wproj, mlp_scale, out):
                 hidden_half(tt, g, 0, square, factor, engines[0], FIRST_0)
             if early_step and s >= FIRST_PROJECT:
                 projects(EARLY_PROJECTS[0], s - 1)
-            if len(queue) > 1:
+            if len(queue) > 1 or (n == 0 and queue and queue[0][6] is not None):
                 quantise_oldest(s)
-            if queue:
+            if queue and queue[-1][6] is None:
                 queue[-1][6] = multiply(queue[-1][1], queue[-1][3], queue[-1][4])
             h_work(s, 4)
             if wf < F_GROUPS:
@@ -460,21 +465,20 @@ def tile_block_pc_kernel(tc, x_mid, wfc, wproj, mlp_scale, out):
             h_work(s, 3)
             if n == 2:
                 hidden_half(tt, g, 1, square, factor, engines[1], FIRST_1 if early_step else FIRST_1_LATE)
-            else:
+            if n == 1:
                 square, factor = hidden_single(tt, g, engines[0])
             if early_step and s >= FIRST_PROJECT:
                 projects(EARLY_PROJECTS[1], s - 1)
             if 0 <= wp < F_GROUPS:
                 quantise_weights(stage_wp, wproj_codes, wproj_scales, wp)
             if not early_step:
-                left = len(steps) - s
-                weight = 2 * (2 * F_GROUPS - s) + F_GROUPS if s < 2 * F_GROUPS else left
-                quota = -(-(len(todo) - TAIL[2 - n]) * (2 if n == 2 else 1) // weight)
-                projects(quota, s - 1)
-            clip_signs(n, factor, engines)
-            queue.append([tt, n, g, square, factor, engines, None])
+                projects(QUOTA[2 - n], s - 1)
+            if n > 0:
+                clip_signs(n, factor, engines)
+                queue.append([tt, n, g, square, factor, engines, None])
+        n = queue[-1][1]
         quantise_oldest(0)
-        queue[-1][6] = multiply(1, queue[-1][3], queue[-1][4])
+        queue[-1][6] = multiply(n, queue[-1][3], queue[-1][4])
         projects(3, 1000)
         quantise_oldest(0)
         projects(1000, 1000)

@@ -24,7 +24,7 @@ GROUP_WORDS = 1024
 RING = (0, 1, 2, 0, 1, 2, 3, 0, 1, 2)
 PAIR_CODES = 14
 RAW_BUFS = 5
-WARM = (5, 0, 2)
+WARM = (0, 0, 0)
 STEP_WARM = ()
 FIRST_0 = False
 FIRST_1_LATE = False
@@ -60,7 +60,7 @@ def tile_block_pc_kernel(tc, x_mid, wfc, wproj, mlp_scale, out):
         act_pool = pools.enter_context(tc.tile_pool(name="act", bufs=4))
         out_pool = pools.enter_context(tc.tile_pool(name="outp", bufs=3))
         psum = pools.enter_context(tc.psum_pool(name="psum", bufs=1))
-        work_banks = list(range(8))
+        work_banks = [2, 3, 4, 5, 6, 7, 0, 1]
 
         def new_bank():
             i = work_banks.pop(0)

from contextlib import ExitStack

import concourse.mybir as mybir
from concourse.masks import make_identity

F32 = mybir.dt.float32
BF16 = mybir.dt.bfloat16
U32 = mybir.dt.uint32
U8 = mybir.dt.uint8
FP8X4 = mybir.dt.float8_e4m3fn_x4
FUNC = mybir.ActivationFunctionType
ALU = mybir.AluOpType

P = 128
T = 640
D = 1024
F = 4096
K_PASS = 512
BANK = 512
D_PASSES = D // K_PASS
F_GROUPS = F // K_PASS
TOKEN_TILES = T // P
GROUP_WORDS = 1024
RING = (0, 1, 2, 0, 1, 2, 3, 0, 1, 2)
PAIR_CODES = 14
RAW_BUFS = 5
WARM = (0, 0, 0)
STEP_WARM = ()
FIRST_0 = False
FIRST_1_LATE = False
FIRST_1 = True
X_AFTER = 7
FIRST_PROJECT = 3
EARLY_PROJECTS = (2, 1)
EARLY = ((0, 0), (0, 1), (1, 0))
WFC_ENGINES = ("scalar", "vector", "scalar", "scalar")
WPROJ_ENGINES = ("scalar", "scalar", "scalar", "vector")
FACTOR_1 = ("vector", "scalar")
FACTOR_2 = (("scalar", "vector"), ("scalar", "scalar"))
FACTOR_3 = ("scalar", "scalar")
QUOTA = (4, 1)
SKIP = ()
Q_PARTS = 2
H_AT = ((2, 2, (4, 4, 5, 6, 7)), (4, 1, (9, 9, 10, 12, 13)))

FLOPS = 2 * 2 * T * D * F


def tile_block_pc_kernel(tc, x_mid, wfc, wproj, mlp_scale, out):
    nc = tc.nc
    x_rows = x_mid.flatten_outer_dims()
    out_rows = out.flatten_outer_dims()

    with ExitStack() as pools:
        pools.enter_context(tc.manual_schedule(engines={mybir.EngineType.PE, mybir.EngineType.Activation}))
        keep = pools.enter_context(tc.tile_pool(name="keep", bufs=1))
        raw_pool = pools.enter_context(tc.tile_pool(name="raw", bufs=RAW_BUFS))
        stage_pool = pools.enter_context(tc.tile_pool(name="stage", bufs=2))
        norm_pool = pools.enter_context(tc.tile_pool(name="norm", bufs=2))
        act_pool = pools.enter_context(tc.tile_pool(name="act", bufs=4))
        out_pool = pools.enter_context(tc.tile_pool(name="outp", bufs=3))
        psum = pools.enter_context(tc.psum_pool(name="psum", bufs=1))
        work_banks = [2, 3, 4, 5, 6, 7, 0, 1]

        def new_bank():
            i = work_banks.pop(0)
            work_banks.append(i)
            bank = psum.tile([P, BANK], F32, name="bank_%d" % i, tag="bank_%d" % i)
            return bank


        x_sb = keep.tile([P, TOKEN_TILES * D], BF16)
        gain = keep.tile([P, D], BF16)
        h_codes = keep.tile([P, TOKEN_TILES * D_PASSES * P], U32, align_bytes=256)
        h_scales = keep.tile([P, TOKEN_TILES * D_PASSES * P], U8, align_bytes=256)
        wfc_codes = keep.tile([P, F_GROUPS * GROUP_WORDS], U32, align_bytes=256)
        wfc_scales = keep.tile([P, F_GROUPS * GROUP_WORDS], U8, align_bytes=256)
        wproj_codes = keep.tile([P, F_GROUPS * GROUP_WORDS], U32, align_bytes=256)
        wproj_scales = keep.tile([P, F_GROUPS * GROUP_WORDS], U8, align_bytes=256)
        sumsq = keep.tile([P, TOKEN_TILES], F32)
        rms = keep.tile([P, TOKEN_TILES], F32)
        rstd = keep.tile([P, TOKEN_TILES], F32)
        eps12 = keep.tile([P, 1], F32)
        warm = keep.tile([P, 1], F32)
        ident_f32 = keep.tile([P, P], F32)

        def load_x(tt):
            nc.sync.dma_start(out=x_sb[:, tt * D : (tt + 1) * D], in_=x_rows[tt * P : (tt + 1) * P, :])

        def words_of(raw):
            words = raw[:].bitcast(F32)
            return [words[:, n * P : (n + 1) * P] for n in range(16)]

        def load_weights(kind, g):
            raw = raw_pool.tile([P, 4 * GROUP_WORDS], BF16, tag="raw")
            if kind == "wfc":
                halves = [slice(0, 2)] if g > 0 else [slice(0, 1), slice(1, 2)]
                for u in halves:
                    nc.sync.dma_start(
                        out=raw[:].rearrange("p (u x) -> p u x", u=2)[:, u, :],
                        in_=wfc[g * K_PASS : (g + 1) * K_PASS, :].rearrange("(u p e) d -> p u (e d)", u=2, e=2)[:, u, :],
                    )
            else:
                nc.sync.dma_start(
                    out=raw[:].rearrange("p (r k) -> p r k", k=K_PASS),
                    in_=wproj[:, g * K_PASS : (g + 1) * K_PASS].rearrange("(r p) k -> p r k", p=P),
                )
            return words_of(raw)

        def square_sum(tt, engine):
            x_tile = x_sb[:, tt * D : (tt + 1) * D]
            squares = norm_pool.tile([P, D], BF16)
            if engine == "scalar":
                nc.scalar.activation(out=squares[:], in_=x_tile, func=FUNC.Square, accum_out=sumsq[:, tt : tt + 1])
            else:
                nc.vector.scalar_tensor_tensor(
                    out=squares[:], in0=x_tile, scalar=1.0, in1=x_tile, op0=ALU.mult, op1=ALU.mult,
                    accum_out=sumsq[:, tt : tt + 1],
                )

        def root(tt, n):
            nc.scalar.activation(
                out=rms[:, tt : tt + n], in_=sumsq[:, tt : tt + n], func=FUNC.Sqrt, scale=12.0 / D, bias=eps12[:]
            )

        def reciprocal(tt, n):
            nc.vector.reciprocal(out=rstd[:, tt : tt + n], in_=rms[:, tt : tt + n])

        def scale_h(tt):
            h_rows = norm_pool.tile([P, D], BF16)
            nc.vector.tensor_scalar(
                out=h_rows[:], in0=x_sb[:, tt * D : (tt + 1) * D], scalar1=rstd[:, tt : tt + 1], scalar2=None, op0=ALU.mult
            )
            return h_rows

        def transpose_h(h_rows):
            words = h_rows[:].bitcast(F32)
            h_bank = new_bank()
            for n in range(4):
                nc.tensor.transpose(h_bank[:, n * P : (n + 1) * P], words[:, n * P : (n + 1) * P], ident_f32[:])
            return h_bank

        def group_h(h_bank, h_grouped, n, ti):
            nc.scalar.copy(
                out=h_grouped[:, 0 : n * D].bitcast(F32).rearrange("p (c i t u) -> p c i t u", c=2, i=n, u=2)[:, :, ti, :, :],
                in_=h_bank[:].rearrange("p (c u t) -> p c t u", c=2, u=2),
            )

        def quantise_h(tt, n, h_grouped):
            cols = slice(tt * 2 * P, (tt + n) * 2 * P)
            nc.vector.quantize_mx(
                out=h_codes[:, cols].bitcast(FP8X4), scales=h_scales[:, cols], in_=h_grouped[:, 0 : n * D]
            )

        def transpose_bank(blocks, b):
            bank = new_bank()
            for i in range(4):
                nc.tensor.transpose(bank[:, i * P : (i + 1) * P], blocks[4 * b + i], ident_f32[:])
            return bank

        def copy_bank(stage, b, bank, engine):
            stage_part = stage[:].bitcast(F32)[:, b * BANK : (b + 1) * BANK].rearrange("p (r m u) -> p r m u", r=2, u=2)
            bank_view = bank[:].rearrange("p (r u m) -> p r m u", r=2, u=2)
            if engine == "scalar":
                nc.scalar.copy(out=stage_part, in_=bank_view)
            else:
                nc.vector.tensor_copy(out=stage_part, in_=bank_view)

        def transpose_weights(blocks, engines):
            stage = stage_pool.tile([P, 4 * GROUP_WORDS], BF16, tag="stage", align_bytes=256)
            banks = [transpose_bank(blocks, b) for b in range(4)]
            for b in range(4):
                copy_bank(stage, b, banks[b], engines[b])
            return stage

        def quantise_weights(stage, codes, scales, g):
            for part in range(Q_PARTS):
                width = GROUP_WORDS // Q_PARTS
                cols = slice(g * GROUP_WORDS + part * width, g * GROUP_WORDS + (part + 1) * width)
                nc.vector.quantize_mx(
                    out=codes[:, cols].bitcast(FP8X4),
                    scales=scales[:, cols],
                    in_=stage[:, part * 4 * width : (part + 1) * 4 * width],
                )

        def hidden_matmul(out, tt, n, g, j):
            for c in range(D_PASSES):
                w_cols = slice(g * GROUP_WORDS + (2 * j + c) * P, g * GROUP_WORDS + (2 * j + c + 1) * P)
                h_cols = slice((2 * tt + c * n) * P, (2 * tt + (c + 1) * n) * P)
                nc.tensor.matmul_mx(
                    out=out,
                    lhsT=wfc_codes[:, w_cols].bitcast(FP8X4),
                    lhsT_scale=wfc_scales[:, w_cols],
                    rhs=h_codes[:, h_cols].bitcast(FP8X4),
                    rhs_scale=h_scales[:, h_cols],
                    start=(c == 0),
                    stop=(c == D_PASSES - 1),
                )

        def take_square(square, words):
            nc.scalar.activation(out=square, in_=words, func=FUNC.Square)

        def take_factor(factor, words, engine):
            if engine == "scalar":
                nc.scalar.activation(out=factor, in_=words, func=FUNC.Sign)
            else:
                nc.vector.tensor_scalar(out=factor, in0=words, scalar1=0.0, scalar2=0.25, op0=ALU.is_ge, op1=ALU.max)

        def hidden_half(tt, g, b, square, factor, engine, factor_first):
            u_bank = new_bank()
            for e in range(2):
                hidden_matmul(u_bank[:, e * 2 * P : (e + 1) * 2 * P], tt, 2, g, 2 * b + e)
            words = u_bank[:].rearrange("p (e t) -> p t e", e=2)
            part = slice(b * BANK, (b + 1) * BANK)
            square_part = square[:, part].rearrange("p (t e) -> p t e", e=2)
            factor_part = factor[:, part].rearrange("p (t e) -> p t e", e=2)
            if factor_first:
                take_factor(factor_part, words, engine)
            take_square(square_part, words)
            if not factor_first:
                take_factor(factor_part, words, engine)

        def hidden_single(tt, g, engine):
            square = act_pool.tile([P, 2 * BANK], BF16, tag="square")
            factor = act_pool.tile([P, 2 * BANK], BF16, tag="factor")
            u_bank = new_bank()
            for j in range(4):
                hidden_matmul(u_bank[:, j * P : (j + 1) * P], tt, 1, g, j)
            words = u_bank[:].rearrange("p (j t) -> p t j", j=4)
            take_square(square[:, 0:BANK].rearrange("p (t j) -> p t j", j=4), words)
            take_factor(factor[:, 0:BANK].rearrange("p (t j) -> p t j", j=4), words, engine)
            return square, factor

        def clip_signs(n, factor, engines):
            for b in range(n):
                if engines[b] == "scalar" and not (b == 1 and engines[0] == "scalar"):
                    last = n if engines == ("scalar", "scalar") else b + 1
                    part = factor[:, b * BANK : last * BANK]
                    nc.vector.tensor_scalar(out=part, in0=part, scalar1=0.25, scalar2=None, op0=ALU.max)

        def multiply(n, square, factor):
            act_grouped = act_pool.tile([P, 2 * BANK], BF16, tag="act_grouped", align_bytes=256)
            if n == 2:
                out_view = act_grouped[:].rearrange("p (t b e) -> p t b e", b=2, e=2)
                square_view = square[:].rearrange("p (b t e) -> p t b e", b=2, e=2)
                factor_view = factor[:].rearrange("p (b t e) -> p t b e", b=2, e=2)
            else:
                out_view, square_view, factor_view = act_grouped[:, 0:BANK], square[:, 0:BANK], factor[:, 0:BANK]
            nc.vector.tensor_tensor(out=out_view, in0=square_view, in1=factor_view, op=ALU.mult)
            return act_grouped

        def quantise_act(n, act_grouped):
            act_codes = act_pool.tile([P, 2 * P], U32, tag="act_codes", align_bytes=256, bufs=PAIR_CODES)
            act_scales = act_pool.tile([P, 2 * P], U8, tag="act_scales", align_bytes=256, bufs=PAIR_CODES)
            nc.vector.quantize_mx(
                out=act_codes[:, 0 : n * P].bitcast(FP8X4), scales=act_scales[:, 0 : n * P], in_=act_grouped[:, 0 : n * BANK]
            )
            return act_codes, act_scales

        sums = {}

        def project(tt, half, g, act):
            act_codes, act_scales = act
            ti = tt % 2
            ring = RING[2 * tt + half]
            if g == 0:
                if ring in work_banks:
                    work_banks.remove(ring)
                sums[(tt, half)] = psum.tile([P, BANK], F32, name="bank_%d" % ring, tag="bank_%d" % ring)
            w_cols = slice(g * GROUP_WORDS + half * BANK, g * GROUP_WORDS + (half + 1) * BANK)
            nc.tensor.matmul_mx(
                out=sums[(tt, half)][:],
                lhsT=act_codes[:, ti * P : (ti + 1) * P].bitcast(FP8X4),
                lhsT_scale=act_scales[:, ti * P : (ti + 1) * P],
                rhs=wproj_codes[:, w_cols].bitcast(FP8X4),
                rhs_scale=wproj_scales[:, w_cols],
                start=(g == 0),
                stop=(g == F_GROUPS - 1),
            )

        results = {}

        def apply_gain(tt, half):
            if half == 0:
                results[tt] = out_pool.tile([P, D], F32, name="result", tag="result")
            pieces = 2 if (tt, half) == (TOKEN_TILES - 1, 1) else 1
            width = BANK // pieces
            for i in range(pieces):
                cols = slice(half * BANK + i * width, half * BANK + (i + 1) * width)
                nc.vector.tensor_tensor(
                    out=results[tt][:, cols],
                    in0=sums[(tt, half)][:, i * width : (i + 1) * width],
                    in1=gain[:, cols],
                    op=ALU.mult,
                )

        def add_residual(tt, first, width):
            cols = slice(first, first + width)
            part = results[tt][:, cols]
            nc.vector.tensor_tensor(
                out=part, in0=part, in1=x_sb[:, tt * D + first : tt * D + first + width], op=ALU.add
            )
            nc.sync.dma_start(out=out_rows[tt * P : (tt + 1) * P, cols], in_=part)

        zeros = keep.tile([P, BANK], BF16)
        nc.gpsimd.memset(zeros[:], 0.0)

        def keep_warm(n):
            if n == 0:
                return
            bank = new_bank()
            for i in range(n):
                nc.tensor.matmul(bank[:], lhsT=zeros[:, 0:P], rhs=zeros[:], start=True, stop=True)

        make_identity(nc, ident_f32[:])
        keep_warm(WARM[0])
        nc.vector.memset(eps12[:], 12.0e-6)
        nc.scalar.activation(out=warm[:], in_=eps12[:], func=FUNC.Sqrt)
        load_order = [("wfc", 0), ("wfc", 1)]
        for g in range(F_GROUPS):
            load_order += [("wfc", g + 2)] if g + 2 < F_GROUPS else []
            load_order += [("wproj", g)]
        blocks = {}

        def load_next():
            if load_order:
                kind, g = load_order.pop(0)
                blocks[(kind, g)] = load_weights(kind, g)
                if len(load_order) == X_AFTER:
                    for tt in range(2, TOKEN_TILES):
                        load_x(tt)
                if not load_order:
                    nc.sync.dma_start(out=gain[:], in_=mlp_scale.partition_broadcast(P))

        load_x(0)
        load_x(1)
        for i in range(RAW_BUFS):
            load_next()
        stage = stage_pool.tile([P, 4 * GROUP_WORDS], BF16, tag="stage", align_bytes=256)
        square_sum(0, "scalar")
        square_sum(1, "vector")
        root(0, 1)
        reciprocal(0, 1)
        h_rows0 = scale_h(0)
        root(1, 1)
        reciprocal(1, 1)
        h_rows1 = scale_h(1)
        banks = [transpose_bank(blocks[("wfc", 0)], b) for b in range(2)]
        bank0 = transpose_h(h_rows0)
        keep_warm(WARM[2])
        bank1 = transpose_h(h_rows1)
        copy_bank(stage, 0, banks[0], "scalar")
        copy_bank(stage, 1, banks[1], "vector")
        h_first = norm_pool.tile([P, 2 * D], BF16, tag="h_grouped", align_bytes=256)
        group_h(bank0, h_first, 2, 0)
        group_h(bank1, h_first, 2, 1)
        banks += [transpose_bank(blocks[("wfc", 0)], b) for b in range(2, 4)]
        load_next()
        half = slice(0, GROUP_WORDS // 2)
        nc.vector.quantize_mx(
            out=wfc_codes[:, half].bitcast(FP8X4), scales=wfc_scales[:, half], in_=stage[:, 0 : 2 * GROUP_WORDS]
        )
        quantise_h(0, 2, h_first)
        keep_warm(WARM[1])
        copy_bank(stage, 2, banks[2], "scalar")
        copy_bank(stage, 3, banks[3], "vector")
        half = slice(GROUP_WORDS // 2, GROUP_WORDS)
        nc.vector.quantize_mx(
            out=wfc_codes[:, half].bitcast(FP8X4), scales=wfc_scales[:, half], in_=stage[:, 2 * GROUP_WORDS :]
        )

        steps = [(tt, n, g) for tt, n in ((0, 2), (2, 2), (4, 1)) for g in range(F_GROUPS)]
        todo = [(tt, half, g) for g in range(F_GROUPS) for tt, half in EARLY]
        for tt in range(4):
            todo += [(tt, half, g) for g in range(F_GROUPS) for half in range(2) if (tt, half) not in EARLY]
        todo += [(4, half, g) for half in range(2) for g in range(F_GROUPS)]
        ready = {}
        gained = []

        def projects(n, step):
            while n > 0 and todo:
                tt, half, g = todo[0]
                if (tt, g) not in ready or ready[(tt, g)][0] > step:
                    return
                todo.pop(0)
                project(tt, half, g, ready[(tt, g)][1])
                n -= 1
                if g == F_GROUPS - 1:
                    apply_gain(tt, half)
                    if (tt, half) == (TOKEN_TILES - 1, 0):
                        gained.append((tt, 0, BANK))
                    elif tt == TOKEN_TILES - 1:
                        gained.extend([(tt, BANK, BANK // 2), (tt, BANK + BANK // 2, BANK // 2)])
                    elif half == 1:
                        gained.append((tt, 0, D))

        h_parts = {}
        queue = []
        stage_wp = None

        def h_work(s, i):
            for t, n, at in H_AT:
                if at[i] != s:
                    continue
                if i == 0:
                    for ti in range(n):
                        square_sum(t + ti, "scalar")
                if i == 1:
                    root(t, n)
                if i == 2:
                    reciprocal(t, n)
                    h_parts[t] = [scale_h(t + ti) for ti in range(n)]
                if i == 3:
                    h_grouped = norm_pool.tile([P, 2 * D], BF16, tag="h_grouped", align_bytes=256)
                    for ti in range(n):
                        group_h(transpose_h(h_parts[t][ti]), h_grouped, n, ti)
                    h_parts[t] = h_grouped
                if i == 4:
                    quantise_h(t, n, h_parts[t])

        def quantise_oldest(s):
            tt, n, g, grouped = queue[0][0], queue[0][1], queue[0][2], queue[0][6]
            queue.pop(0)
            act = quantise_act(n, grouped)
            for ti in range(n):
                ready[(tt + ti, g)] = (s, act)

        plan = []
        left = list(steps)
        while left or len(plan) <= F_GROUPS:
            plan.append(None if len(plan) in SKIP or not left else left.pop(0))
        for s in range(len(plan)):
            wf = s + 1
            wp = s - 1
            early_step = s < F_GROUPS
            tt, n, g = plan[s] or (0, 0, 0)
            engines = FACTOR_1 if early_step else (FACTOR_2[s % 2] if n == 2 else (FACTOR_3[s % 2],))
            if n == 2:
                square = act_pool.tile([P, 2 * BANK], BF16, tag="square")
                factor = act_pool.tile([P, 2 * BANK], BF16, tag="factor")
            if wf < F_GROUPS:
                stage = transpose_weights(blocks[("wfc", wf)], WFC_ENGINES)
                load_next()
            h_work(s, 2)
            if s < len(STEP_WARM):
                keep_warm(STEP_WARM[s])
            if n == 2:
                hidden_half(tt, g, 0, square, factor, engines[0], FIRST_0)
            if early_step and s >= FIRST_PROJECT:
                projects(EARLY_PROJECTS[0], s - 1)
            if len(queue) > 1 or (n == 0 and queue and queue[0][6] is not None):
                quantise_oldest(s)
            if queue and queue[-1][6] is None:
                queue[-1][6] = multiply(queue[-1][1], queue[-1][3], queue[-1][4])
            h_work(s, 4)
            if wf < F_GROUPS:
                quantise_weights(stage, wfc_codes, wfc_scales, wf)
            while gained:
                add_residual(*gained.pop(0))
            h_work(s, 0)
            h_work(s, 1)
            if 0 <= wp < F_GROUPS:
                stage_wp = transpose_weights(blocks[("wproj", wp)], WPROJ_ENGINES)
                load_next()
            h_work(s, 3)
            if n == 2:
                hidden_half(tt, g, 1, square, factor, engines[1], FIRST_1 if early_step else FIRST_1_LATE)
            if n == 1:
                square, factor = hidden_single(tt, g, engines[0])
            if early_step and s >= FIRST_PROJECT:
                projects(EARLY_PROJECTS[1], s - 1)
            if 0 <= wp < F_GROUPS:
                quantise_weights(stage_wp, wproj_codes, wproj_scales, wp)
            if not early_step:
                projects(QUOTA[2 - n], s - 1)
            if n > 0:
                clip_signs(n, factor, engines)
                queue.append([tt, n, g, square, factor, engines, None])
        n = queue[-1][1]
        quantise_oldest(0)
        queue[-1][6] = multiply(n, queue[-1][3], queue[-1][4])
        projects(3, 1000)
        quantise_oldest(0)
        projects(1000, 1000)
        while gained:
            add_residual(*gained.pop(0))
